import numpy as np
import ml_dtypes

BF16 = ml_dtypes.bfloat16


def bf(x):
    return np.asarray(x, np.float32).astype(BF16)


def f32(x):
    return np.asarray(x, np.float32)


def f64(x):
    return np.asarray(x).astype(np.float64)


def striped(idx):
    return np.tile(idx.reshape(-1, 16).T, (8, 1))


D, V, T, B, N = 128, 4096, 1024, 2, 2048
BETA1 = 2.0 ** -12
SC1 = np.sqrt(T) * ((V + T) / T) ** 2 * BETA1


def setup_inputs():
    return {
        "table": bf(np.random.standard_normal((D, V))),
        "pos": bf(0.5 * np.random.standard_normal((T, T))),
        "wq1": bf(np.random.standard_normal((T, T)) / np.sqrt(T)),
        "wk1": bf(np.random.standard_normal((T, T)) / np.sqrt(T)),
        "wv1": bf(np.random.standard_normal((D, D)) / np.sqrt(D)),
        "wv2": bf(np.random.standard_normal((D, D)) / np.sqrt(D)),
        "offs": striped(np.random.permutation(np.tile(np.arange(V), 2))[:N]),
    }


def reference(table, pos, wq1, wk1, wv1, wv2, offs):
    idx = offs[:16].T.reshape(-1)
    e = f64(table)[:, idx]
    q1 = f64(wq1).T @ f64(pos)
    k1 = f64(wk1).T @ f64(pos)
    s1 = SC1 * (q1.T @ k1)
    keep = np.tril(np.ones((T, T), bool))
    s1 = np.where(keep, s1, -np.inf)
    a1 = np.exp(s1 - s1.max(axis=1, keepdims=True))
    a1 = a1 / a1.sum(axis=1, keepdims=True)
    a1[0, :] = 0.0
    v1 = f64(wv1).T @ e
    y1 = np.concatenate([v1[:, i * T:(i + 1) * T] @ a1.T for i in range(B)], axis=1)
    return np.concatenate([e + y1, f64(wv2).T @ e], axis=0)

@@ -1,0 +1,218 @@
+import concourse.mybir as mybir
+from concourse.masks import make_identity
+
+BF16 = mybir.dt.bfloat16
+F32 = mybir.dt.float32
+U16 = mybir.dt.uint16
+I32 = mybir.dt.int32
+EXP = mybir.ActivationFunctionType.Exp
+IS_GT = mybir.AluOpType.is_gt
+MULT = mybir.AluOpType.mult
+X = mybir.AxisListType.X
+
+P = 128
+V = 4096
+T = 1024
+B = 2
+N = B * T
+NB = T // P
+BANK = 512
+CHUNKS = T // BANK
+CHUNK_BLOCKS = BANK // P
+PIECE_COLS = BANK // 16
+SCALE = 0.1953125
+MASKED = -1.0e30
+
+CAUSAL_PAIRS = T * (T + 1) // 2
+FLOPS = 2 * (2 * T * T * T + T * CAUSAL_PAIRS + B * P * CAUSAL_PAIRS + 2 * P * P * N)
+
+
+def tile_inductionheadattentionsmaller_b_kernel(tc, table, pos, wq1, wk1, wv1, wv2, offs, out):
+    nc = tc.nc
+
+    def copy_out(turn, dst, src):
+        if turn % 2 == 0:
+            nc.vector.tensor_copy(dst, src)
+        else:
+            nc.scalar.copy(dst, src)
+
+    with (
+        tc.tile_pool(name="held", bufs=1) as held,
+        tc.tile_pool(name="work", bufs=3) as work,
+        tc.tile_pool(name="stats", bufs=4) as stats,
+        tc.tile_pool(name="staging", bufs=4) as staging,
+    ):
+        offsets = held.tile([P, N // 16], U16, name="offsets")
+        nc.sync.dma_start(offsets[:], offs)
+        pos_sb = [held.tile([P, T], BF16, name=f"pos_sb{f}") for f in range(NB)]
+        wq_sb = [held.tile([P, T], BF16, name=f"wq_sb{f}") for f in range(NB)]
+        wk_sb = [held.tile([P, T], BF16, name=f"wk_sb{f}") for f in range(NB)]
+        for f in range(NB):
+            nc.sync.dma_start(pos_sb[f][:], pos[f * P : (f + 1) * P, :])
+            nc.scalar.dma_start(wq_sb[f][:], wq1[f * P : (f + 1) * P, :])
+        for f in range(NB):
+            queue = nc.sync if f % 2 == 0 else nc.scalar
+            queue.dma_start(wk_sb[f][:], wk1[f * P : (f + 1) * P, :])
+        table_sb = held.tile([P, V], BF16, name="table_sb")
+        nc.sync.dma_start(table_sb[:], table)
+        wv1_sb = held.tile([P, P], BF16, name="wv1_sb")
+        nc.scalar.dma_start(wv1_sb[:], wv1)
+        wv2_sb = held.tile([P, P], BF16, name="wv2_sb")
+        nc.scalar.dma_start(wv2_sb[:], wv2)
+
+        ident = held.tile([P, P], BF16, name="ident")
+        make_identity(nc, ident[:])
+        u_minus_t = held.tile([P, P], I32, name="u_minus_t")
+        nc.gpsimd.iota(u_minus_t[:], pattern=[[1, P]], base=0, channel_multiplier=-1)
+        above_diag = held.tile([P, P], BF16, name="above_diag")
+        nc.vector.tensor_scalar(above_diag[:], u_minus_t[:], 0.0, MASKED, op0=IS_GT, op1=MULT)
+
+        q_sb = [held.tile([P, T], BF16, name=f"q_sb{a}") for a in range(NB)]
+        k_sb = [held.tile([P, T], BF16, name=f"k_sb{a}") for a in range(NB)]
+        with tc.psum_pool(name="proj_psum", bufs=1) as proj_psum:
+            for w_sb, proj_sb in ((wq_sb, q_sb), (wk_sb, k_sb)):
+                for a0 in range(0, NB, 4):
+                    spots = [(a, c) for a in range(a0, a0 + 4) for c in range(CHUNKS)]
+                    acc = [proj_psum.tile([P, BANK], F32, name=f"acc{n}") for n in range(len(spots))]
+                    for f in range(NB):
+                        for n, (a, c) in enumerate(spots):
+                            nc.tensor.matmul(
+                                acc[n][:],
+                                lhsT=w_sb[f][:, a * P : (a + 1) * P],
+                                rhs=pos_sb[f][:, c * BANK : (c + 1) * BANK],
+                                start=(f == 0),
+                                stop=(f == NB - 1),
+                            )
+                    for n, (a, c) in enumerate(spots):
+                        copy_out(n, proj_sb[a][:, c * BANK : (c + 1) * BANK], acc[n][:])
+
+        with (
+            tc.psum_pool(name="s_psum", bufs=4) as s_psum,
+            tc.psum_pool(name="t_psum", bufs=2) as t_psum,
+            tc.psum_pool(name="y_psum", bufs=1) as y_psum,
+        ):
+
+            def looked_up(piece):
+                return table_sb[:].indirect(offsets[:, piece * PIECE_COLS : (piece + 1) * PIECE_COLS])
+
+            v1_sb = held.tile([P, N], BF16, name="v1_sb")
+            for piece in range(N // BANK):
+                v1_ps = s_psum.tile([P, BANK], F32, name="s_ps")
+                nc.tensor.matmul(v1_ps[:], lhsT=wv1_sb[:], rhs=looked_up(piece), start=True, stop=True)
+                copy_out(piece, v1_sb[:, piece * BANK : (piece + 1) * BANK], v1_ps[:])
+            for piece in range(N // BANK):
+                v2_ps = s_psum.tile([P, BANK], F32, name="s_ps")
+                nc.tensor.matmul(v2_ps[:], lhsT=wv2_sb[:], rhs=looked_up(piece), start=True, stop=True)
+                v2_sb = staging.tile([P, BANK], F32, name="staged")
+                copy_out(piece, v2_sb[:], v2_ps[:])
+                nc.sync.dma_start(out[P : 2 * P, piece * BANK : (piece + 1) * BANK], v2_sb[:])
+
+            def start_chunk(c):
+                y = y_psum.tile([P, B, BANK], F32, name="y")
+                for s in range(B):
+                    nc.tensor.matmul(
+                        y[:, s, :], lhsT=ident[:], rhs=looked_up(s * CHUNKS + c), start=True, stop=False
+                    )
+                return y
+
+            def finish_chunk(c, y):
+                for s in range(B):
+                    y_sb = staging.tile([P, BANK], F32, name="staged")
+                    copy_out(s, y_sb[:], y[:, s, :])
+                    nc.sync.dma_start(out[0:P, s * T + c * BANK : s * T + (c + 1) * BANK], y_sb[:])
+
+            y = start_chunk(CHUNKS - 1)
+
+            v1T = held.tile([P, B * NB, P], BF16, name="v1T")
+            for s in range(B):
+                v1T_ps = t_psum.tile([P, T], BF16, name="t_ps")
+                for k in range(NB):
+                    j = (s * NB + k) * P
+                    nc.tensor.transpose(v1T_ps[:, k * P : (k + 1) * P], v1_sb[:, j : j + P], ident[:])
+                copy_out(s, v1T[:, s * NB : (s + 1) * NB, :], v1T_ps[:].rearrange("p (k m) -> p k m", m=P))
+
+            def scores(i):
+                width = (i + 1) * P
+                pieces = []
+                for lo in range(0, width, BANK):
+                    hi = min(lo + BANK, width)
+                    has_diagonal = hi == width
+                    s_ps = s_psum.tile([P, BANK], F32, name="s_ps")
+                    for a in range(NB):
+                        nc.tensor.matmul(
+                            s_ps[:, : hi - lo],
+                            lhsT=q_sb[a][:, i * P : (i + 1) * P],
+                            rhs=k_sb[a][:, lo:hi],
+                            start=(a == 0),
+                            stop=(a == NB - 1 and not has_diagonal),
+                        )
+                    if has_diagonal:
+                        nc.tensor.matmul(
+                            s_ps[:, hi - lo - P : hi - lo], lhsT=ident[:], rhs=above_diag[:], start=False, stop=True
+                        )
+                    pieces.append((lo, hi, s_ps))
+                return pieces
+
+            def softmax(i, pieces):
+                width = (i + 1) * P
+                n = len(pieces)
+                piece_max = stats.tile([P, CHUNKS], F32, name="piece_max")
+                for p, (lo, hi, s_ps) in enumerate(pieces):
+                    nc.vector.reduce_max(out=piece_max[:, p : p + 1], in_=s_ps[:, : hi - lo], axis=X)
+                row_max = stats.tile([P, 1], F32, name="row_max")
+                nc.vector.reduce_max(out=row_max[:], in_=piece_max[:, :n], axis=X)
+                shift = stats.tile([P, 1], F32, name="shift")
+                nc.vector.tensor_scalar_mul(shift[:], row_max[:], -SCALE)
+                expd = work.tile([P, T], F32, name="expd")
+                piece_sum = stats.tile([P, CHUNKS], F32, name="piece_sum")
+                for p, (lo, hi, s_ps) in enumerate(pieces):
+                    nc.scalar.activation(
+                        out=expd[:, lo:hi],
+                        in_=s_ps[:, : hi - lo],
+                        func=EXP,
+                        bias=shift[:],
+                        scale=SCALE,
+                        accum_out=piece_sum[:, p : p + 1],
+                    )
+                row_sum = stats.tile([P, 1], F32, name="row_sum")
+                nc.vector.reduce_sum(out=row_sum[:], in_=piece_sum[:, :n], axis=X)
+                inv_sum = stats.tile([P, 1], F32, name="inv_sum")
+                nc.vector.reciprocal(inv_sum[:], row_sum[:])
+                if i == 0:
+                    nc.vector.memset(inv_sum[0:1, :], 0.0)
+                a1 = work.tile([P, T], BF16, name="a1")
+                nc.vector.tensor_scalar_mul(a1[:, :width], expd[:, :width], inv_sum[:])
+                return a1
+
+            def mix(i, a1, y):
+                width = (i + 1) * P
+                a1T_ps = t_psum.tile([P, T], BF16, name="t_ps")
+                for k in range(i + 1):
+                    nc.tensor.transpose(a1T_ps[:, k * P : (k + 1) * P], a1[:, k * P : (k + 1) * P], ident[:])
+                a1T = work.tile([P, T], BF16, name="a1T")
+                nc.scalar.copy(a1T[:, :width], a1T_ps[:, :width])
+                col = (i % CHUNK_BLOCKS) * P
+                last_block = i % CHUNK_BLOCKS == 0
+                for s in range(B):
+                    for k in range(i + 1):
+                        nc.tensor.matmul(
+                            y[:, s, col : col + P],
+                            lhsT=v1T[:, s * NB + k, :],
+                            rhs=a1T[:, k * P : (k + 1) * P],
+                            start=False,
+                            stop=(last_block and k == i),
+                        )
+
+            AHEAD = 2
+            a1_of = {}
+            for i in range(NB - 1, NB - 1 - AHEAD, -1):
+                a1_of[i] = softmax(i, scores(i))
+            for i in range(NB - 1, -1, -1):
+                if i - AHEAD >= 0:
+                    a1_of[i - AHEAD] = softmax(i - AHEAD, scores(i - AHEAD))
+                mix(i, a1_of[i], y)
+                if i % CHUNK_BLOCKS == 0:
+                    c = i // CHUNK_BLOCKS
+                    finish_chunk(c, y)
+                    if c > 0:
+                        y = start_chunk(c - 1)

@@ -8,6 +8,7 @@ I32 = mybir.dt.int32
 EXP = mybir.ActivationFunctionType.Exp
 IS_GT = mybir.AluOpType.is_gt
 MULT = mybir.AluOpType.mult
+MAX = mybir.AluOpType.max
 X = mybir.AxisListType.X
 
 P = 128
@@ -17,11 +18,18 @@ B = 2
 N = B * T
 NB = T // P
 BANK = 512
+BANK_BYTES = 4 * BANK
+BANKS = 8
 CHUNKS = T // BANK
 CHUNK_BLOCKS = BANK // P
 PIECE_COLS = BANK // 16
 SCALE = 0.1953125
+WARM_UP_MATMULS = 16
 MASKED = -1.0e30
+
+Y_BANK = 0
+T_BANKS = (2, 3)
+S_BANKS = ((6, 7), (4, 5))
 
 CAUSAL_PAIRS = T * (T + 1) // 2
 FLOPS = 2 * (2 * T * T * T + T * CAUSAL_PAIRS + B * P * CAUSAL_PAIRS + 2 * P * P * N)
@@ -38,21 +46,35 @@ def tile_inductionheadattentionsmaller_b_kernel(tc, table, pos, wq1, wk1, wv1, w
 
     with (
         tc.tile_pool(name="held", bufs=1) as held,
-        tc.tile_pool(name="work", bufs=3) as work,
+        tc.tile_pool(name="work", bufs=4) as work,
         tc.tile_pool(name="stats", bufs=4) as stats,
         tc.tile_pool(name="staging", bufs=4) as staging,
+        tc.psum_pool(name="psum", bufs=1) as psum,
     ):
-        offsets = held.tile([P, N // 16], U16, name="offsets")
-        nc.sync.dma_start(offsets[:], offs)
+
+        def bank_f32(b):
+            return psum.tile([P, BANK], F32, name=f"f32_bank{b}", offset=b * BANK_BYTES)
+
+        def bank_bf16(b):
+            return psum.tile([P, 2 * BANK], BF16, name=f"bf16_bank{b}", offset=b * BANK_BYTES)
+
+        zeros = held.tile([P, P], BF16, name="zeros")
+        nc.gpsimd.memset(zeros[:], 0.0)
+        warm_ps = bank_f32(BANKS - 1)
+        for n in range(WARM_UP_MATMULS):
+            nc.tensor.matmul(warm_ps[:, 0:P], lhsT=zeros[:], rhs=zeros[:], start=True, stop=True)
+
         pos_sb = [held.tile([P, T], BF16, name=f"pos_sb{f}") for f in range(NB)]
-        wq_sb = [held.tile([P, T], BF16, name=f"wq_sb{f}") for f in range(NB)]
         wk_sb = [held.tile([P, T], BF16, name=f"wk_sb{f}") for f in range(NB)]
+        wq_sb = [held.tile([P, T], BF16, name=f"wq_sb{f}") for f in range(NB)]
         for f in range(NB):
             nc.sync.dma_start(pos_sb[f][:], pos[f * P : (f + 1) * P, :])
-            nc.scalar.dma_start(wq_sb[f][:], wq1[f * P : (f + 1) * P, :])
+            nc.scalar.dma_start(wk_sb[f][:], wk1[f * P : (f + 1) * P, :])
         for f in range(NB):
             queue = nc.sync if f % 2 == 0 else nc.scalar
-            queue.dma_start(wk_sb[f][:], wk1[f * P : (f + 1) * P, :])
+            queue.dma_start(wq_sb[f][:], wq1[f * P : (f + 1) * P, :])
+        offsets = held.tile([P, N // 16], U16, name="offsets")
+        nc.sync.dma_start(offsets[:], offs)
         table_sb = held.tile([P, V], BF16, name="table_sb")
         nc.sync.dma_start(table_sb[:], table)
         wv1_sb = held.tile([P, P], BF16, name="wv1_sb")
@@ -67,152 +89,175 @@ def tile_inductionheadattentionsmaller_b_kernel(tc, table, pos, wq1, wk1, wv1, w
         above_diag = held.tile([P, P], BF16, name="above_diag")
         nc.vector.tensor_scalar(above_diag[:], u_minus_t[:], 0.0, MASKED, op0=IS_GT, op1=MULT)
 
-        q_sb = [held.tile([P, T], BF16, name=f"q_sb{a}") for a in range(NB)]
-        k_sb = [held.tile([P, T], BF16, name=f"k_sb{a}") for a in range(NB)]
-        with tc.psum_pool(name="proj_psum", bufs=1) as proj_psum:
-            for w_sb, proj_sb in ((wq_sb, q_sb), (wk_sb, k_sb)):
-                for a0 in range(0, NB, 4):
-                    spots = [(a, c) for a in range(a0, a0 + 4) for c in range(CHUNKS)]
-                    acc = [proj_psum.tile([P, BANK], F32, name=f"acc{n}") for n in range(len(spots))]
-                    for f in range(NB):
-                        for n, (a, c) in enumerate(spots):
-                            nc.tensor.matmul(
-                                acc[n][:],
-                                lhsT=w_sb[f][:, a * P : (a + 1) * P],
-                                rhs=pos_sb[f][:, c * BANK : (c + 1) * BANK],
-                                start=(f == 0),
-                                stop=(f == NB - 1),
-                            )
-                    for n, (a, c) in enumerate(spots):
-                        copy_out(n, proj_sb[a][:, c * BANK : (c + 1) * BANK], acc[n][:])
+        not_row0 = held.tile([P, 1], F32, name="not_row0")
+        nc.vector.memset(not_row0[:], 1.0)
+        nc.vector.memset(not_row0[0:1, :], 0.0)
 
-        with (
-            tc.psum_pool(name="s_psum", bufs=4) as s_psum,
-            tc.psum_pool(name="t_psum", bufs=2) as t_psum,
-            tc.psum_pool(name="y_psum", bufs=1) as y_psum,
-        ):
+        q_sb = [[held.tile([P, BANK], BF16, name=f"q_sb{a}_{c}") for c in range(CHUNKS)] for a in range(NB)]
+        k_sb = [[held.tile([P, BANK], BF16, name=f"k_sb{a}_{c}") for c in range(CHUNKS)] for a in range(NB)]
 
-            def looked_up(piece):
-                return table_sb[:].indirect(offsets[:, piece * PIECE_COLS : (piece + 1) * PIECE_COLS])
+        def project_step(acc, w_sb, a, c, f):
+            nc.tensor.matmul(
+                acc[:],
+                lhsT=w_sb[f][:, a * P : (a + 1) * P],
+                rhs=pos_sb[f][:, c * BANK : (c + 1) * BANK],
+                start=(f == 0),
+                stop=(f == NB - 1),
+            )
 
-            v1_sb = held.tile([P, N], BF16, name="v1_sb")
-            for piece in range(N // BANK):
-                v1_ps = s_psum.tile([P, BANK], F32, name="s_ps")
-                nc.tensor.matmul(v1_ps[:], lhsT=wv1_sb[:], rhs=looked_up(piece), start=True, stop=True)
-                copy_out(piece, v1_sb[:, piece * BANK : (piece + 1) * BANK], v1_ps[:])
-            for piece in range(N // BANK):
-                v2_ps = s_psum.tile([P, BANK], F32, name="s_ps")
-                nc.tensor.matmul(v2_ps[:], lhsT=wv2_sb[:], rhs=looked_up(piece), start=True, stop=True)
-                v2_sb = staging.tile([P, BANK], F32, name="staged")
-                copy_out(piece, v2_sb[:], v2_ps[:])
-                nc.sync.dma_start(out[P : 2 * P, piece * BANK : (piece + 1) * BANK], v2_sb[:])
+        def project_together(w_sb, proj_sb, c):
+            accs = [bank_f32(a) for a in range(NB)]
+            for f in range(NB):
+                for a in range(NB):
+                    project_step(accs[a], w_sb, a, c, f)
+            for a in range(NB):
+                copy_out(a, proj_sb[a][c][:], accs[a][:])
 
-            def start_chunk(c):
-                y = y_psum.tile([P, B, BANK], F32, name="y")
-                for s in range(B):
-                    nc.tensor.matmul(
-                        y[:, s, :], lhsT=ident[:], rhs=looked_up(s * CHUNKS + c), start=True, stop=False
-                    )
-                return y
+        def project_in_turn(w_sb, proj_sb, c, banks):
+            for a in range(NB):
+                acc = bank_f32(banks[a % len(banks)])
+                for f in range(NB):
+                    project_step(acc, w_sb, a, c, f)
+                copy_out(a, proj_sb[a][c][:], acc[:])
 
-            def finish_chunk(c, y):
-                for s in range(B):
-                    y_sb = staging.tile([P, BANK], F32, name="staged")
-                    copy_out(s, y_sb[:], y[:, s, :])
-                    nc.sync.dma_start(out[0:P, s * T + c * BANK : s * T + (c + 1) * BANK], y_sb[:])
+        project_together(wk_sb, k_sb, 0)
+        project_in_turn(wk_sb, k_sb, 1, range(BANKS))
+        project_in_turn(wq_sb, q_sb, 1, range(BANKS))
+        project_in_turn(wq_sb, q_sb, 0, range(BANKS))
 
-            y = start_chunk(CHUNKS - 1)
+        def looked_up(piece):
+            return table_sb[:].indirect(offsets[:, piece * PIECE_COLS : (piece + 1) * PIECE_COLS])
 
-            v1T = held.tile([P, B * NB, P], BF16, name="v1T")
+        def start_chunk(c):
+            y = psum.tile([P, B, BANK], F32, name="y", offset=Y_BANK * BANK_BYTES)
             for s in range(B):
-                v1T_ps = t_psum.tile([P, T], BF16, name="t_ps")
+                nc.tensor.matmul(y[:, s, :], lhsT=ident[:], rhs=looked_up(s * CHUNKS + c), start=True, stop=False)
+            return y
+
+        def finish_chunk(c, y):
+            for s in range(B):
+                y_sb = staging.tile([P, BANK], F32, name="staged")
+                copy_out(s, y_sb[:], y[:, s, :])
+                queue = nc.sync if s % 2 == 0 else nc.scalar
+                queue.dma_start(out[0:P, s * T + c * BANK : s * T + (c + 1) * BANK], y_sb[:])
+
+        v1_sb = held.tile([P, N], BF16, name="v1_sb")
+        for piece in range(N // BANK):
+            v1_ps = bank_f32(2 + piece)
+            nc.tensor.matmul(v1_ps[:], lhsT=wv1_sb[:], rhs=looked_up(piece), start=True, stop=True)
+            copy_out(piece, v1_sb[:, piece * BANK : (piece + 1) * BANK], v1_ps[:])
+        y = start_chunk(CHUNKS - 1)
+        for piece in range(N // BANK):
+            v2_ps = bank_f32(2 + (N // BANK + piece) % 6)
+            nc.tensor.matmul(v2_ps[:], lhsT=wv2_sb[:], rhs=looked_up(piece), start=True, stop=True)
+            v2_sb = staging.tile([P, BANK], F32, name="staged")
+            copy_out(piece, v2_sb[:], v2_ps[:])
+            nc.sync.dma_start(out[P : 2 * P, piece * BANK : (piece + 1) * BANK], v2_sb[:])
+
+        v1T = held.tile([P, B * NB, P], BF16, name="v1T")
+
+        def transpose_v1():
+            for s in range(B):
+                v1T_ps = bank_bf16(T_BANKS[s])
                 for k in range(NB):
                     j = (s * NB + k) * P
                     nc.tensor.transpose(v1T_ps[:, k * P : (k + 1) * P], v1_sb[:, j : j + P], ident[:])
                 copy_out(s, v1T[:, s * NB : (s + 1) * NB, :], v1T_ps[:].rearrange("p (k m) -> p k m", m=P))
 
-            def scores(i):
-                width = (i + 1) * P
-                pieces = []
-                for lo in range(0, width, BANK):
-                    hi = min(lo + BANK, width)
-                    has_diagonal = hi == width
-                    s_ps = s_psum.tile([P, BANK], F32, name="s_ps")
-                    for a in range(NB):
-                        nc.tensor.matmul(
-                            s_ps[:, : hi - lo],
-                            lhsT=q_sb[a][:, i * P : (i + 1) * P],
-                            rhs=k_sb[a][:, lo:hi],
-                            start=(a == 0),
-                            stop=(a == NB - 1 and not has_diagonal),
-                        )
-                    if has_diagonal:
-                        nc.tensor.matmul(
-                            s_ps[:, hi - lo - P : hi - lo], lhsT=ident[:], rhs=above_diag[:], start=False, stop=True
-                        )
-                    pieces.append((lo, hi, s_ps))
-                return pieces
-
-            def softmax(i, pieces):
-                width = (i + 1) * P
-                n = len(pieces)
-                piece_max = stats.tile([P, CHUNKS], F32, name="piece_max")
-                for p, (lo, hi, s_ps) in enumerate(pieces):
-                    nc.vector.reduce_max(out=piece_max[:, p : p + 1], in_=s_ps[:, : hi - lo], axis=X)
-                row_max = stats.tile([P, 1], F32, name="row_max")
-                nc.vector.reduce_max(out=row_max[:], in_=piece_max[:, :n], axis=X)
-                shift = stats.tile([P, 1], F32, name="shift")
-                nc.vector.tensor_scalar_mul(shift[:], row_max[:], -SCALE)
-                expd = work.tile([P, T], F32, name="expd")
-                piece_sum = stats.tile([P, CHUNKS], F32, name="piece_sum")
-                for p, (lo, hi, s_ps) in enumerate(pieces):
-                    nc.scalar.activation(
-                        out=expd[:, lo:hi],
-                        in_=s_ps[:, : hi - lo],
-                        func=EXP,
-                        bias=shift[:],
-                        scale=SCALE,
-                        accum_out=piece_sum[:, p : p + 1],
+        def scores(i, banks):
+            width = (i + 1) * P
+            col = (i % CHUNK_BLOCKS) * P
+            pieces = []
+            for p, lo in enumerate(range(0, width, BANK)):
+                hi = min(lo + BANK, width)
+                has_diagonal = hi == width
+                s_ps = bank_f32(banks[p])
+                for a in range(NB):
+                    nc.tensor.matmul(
+                        s_ps[:, : hi - lo],
+                        lhsT=q_sb[a][i // CHUNK_BLOCKS][:, col : col + P],
+                        rhs=k_sb[a][p][:, : hi - lo],
+                        start=(a == 0),
+                        stop=(a == NB - 1 and not has_diagonal),
                     )
+                if has_diagonal:
+                    nc.tensor.matmul(
+                        s_ps[:, hi - lo - P : hi - lo], lhsT=ident[:], rhs=above_diag[:], start=False, stop=True
+                    )
+                pieces.append((lo, hi, s_ps))
+            return pieces
+
+        def softmax(i, pieces):
+            width = (i + 1) * P
+            two_pieces = len(pieces) == 2
+            piece_max = stats.tile([P, CHUNKS], F32, name="piece_max")
+            for p, (lo, hi, s_ps) in enumerate(pieces):
+                nc.vector.reduce_max(out=piece_max[:, p : p + 1], in_=s_ps[:, : hi - lo], axis=X)
+            shift = stats.tile([P, 1], F32, name="shift")
+            if two_pieces:
+                nc.vector.tensor_scalar(shift[:], piece_max[:, 0:1], piece_max[:, 1:2], -SCALE, op0=MAX, op1=MULT)
+            else:
+                nc.vector.tensor_scalar_mul(shift[:], piece_max[:, 0:1], -SCALE)
+            expd = work.tile([P, T], F32, name="expd")
+            piece_sum = stats.tile([P, CHUNKS], F32, name="piece_sum")
+            for p, (lo, hi, s_ps) in enumerate(pieces):
+                nc.scalar.activation(
+                    out=expd[:, lo:hi],
+                    in_=s_ps[:, : hi - lo],
+                    func=EXP,
+                    bias=shift[:],
+                    scale=SCALE,
+                    accum_out=piece_sum[:, p : p + 1],
+                )
+            inv_sum = stats.tile([P, 1], F32, name="inv_sum")
+            if two_pieces:
                 row_sum = stats.tile([P, 1], F32, name="row_sum")
-                nc.vector.reduce_sum(out=row_sum[:], in_=piece_sum[:, :n], axis=X)
-                inv_sum = stats.tile([P, 1], F32, name="inv_sum")
+                nc.vector.tensor_add(row_sum[:], piece_sum[:, 0:1], piece_sum[:, 1:2])
                 nc.vector.reciprocal(inv_sum[:], row_sum[:])
-                if i == 0:
-                    nc.vector.memset(inv_sum[0:1, :], 0.0)
-                a1 = work.tile([P, T], BF16, name="a1")
+            else:
+                nc.vector.reciprocal(inv_sum[:], piece_sum[:, 0:1])
+            a1 = work.tile([P, T], BF16, name="a1")
+            if i == 0:
+                nc.vector.tensor_scalar(a1[:, :width], expd[:, :width], inv_sum[:], not_row0[:], op0=MULT, op1=MULT)
+            else:
                 nc.vector.tensor_scalar_mul(a1[:, :width], expd[:, :width], inv_sum[:])
-                return a1
+            return a1
 
-            def mix(i, a1, y):
-                width = (i + 1) * P
-                a1T_ps = t_psum.tile([P, T], BF16, name="t_ps")
+        def transposed(i, a1):
+            width = (i + 1) * P
+            a1T_ps = bank_bf16(T_BANKS[i % 2])
+            for k in range(i + 1):
+                nc.tensor.transpose(a1T_ps[:, k * P : (k + 1) * P], a1[:, k * P : (k + 1) * P], ident[:])
+            a1T = work.tile([P, T], BF16, name="a1T")
+            nc.scalar.copy(a1T[:, :width], a1T_ps[:, :width])
+            return a1T
+
+        def mix(i, a1T, y):
+            col = (i % CHUNK_BLOCKS) * P
+            last_block = i % CHUNK_BLOCKS == 0
+            for s in range(B):
                 for k in range(i + 1):
-                    nc.tensor.transpose(a1T_ps[:, k * P : (k + 1) * P], a1[:, k * P : (k + 1) * P], ident[:])
-                a1T = work.tile([P, T], BF16, name="a1T")
-                nc.scalar.copy(a1T[:, :width], a1T_ps[:, :width])
-                col = (i % CHUNK_BLOCKS) * P
-                last_block = i % CHUNK_BLOCKS == 0
-                for s in range(B):
-                    for k in range(i + 1):
-                        nc.tensor.matmul(
-                            y[:, s, col : col + P],
-                            lhsT=v1T[:, s * NB + k, :],
-                            rhs=a1T[:, k * P : (k + 1) * P],
-                            start=False,
-                            stop=(last_block and k == i),
-                        )
+                    nc.tensor.matmul(
+                        y[:, s, col : col + P],
+                        lhsT=v1T[:, s * NB + k, :],
+                        rhs=a1T[:, k * P : (k + 1) * P],
+                        start=False,
+                        stop=(last_block and k == i),
+                    )
 
-            AHEAD = 2
-            a1_of = {}
-            for i in range(NB - 1, NB - 1 - AHEAD, -1):
-                a1_of[i] = softmax(i, scores(i))
-            for i in range(NB - 1, -1, -1):
-                if i - AHEAD >= 0:
-                    a1_of[i - AHEAD] = softmax(i - AHEAD, scores(i - AHEAD))
-                mix(i, a1_of[i], y)
-                if i % CHUNK_BLOCKS == 0:
-                    c = i // CHUNK_BLOCKS
-                    finish_chunk(c, y)
-                    if c > 0:
-                        y = start_chunk(c - 1)
+        a1_of = {}
+        a1T_of = {}
+        for step in range(NB + 3):
+            i = NB - 1 - step
+            if 0 <= i:
+                a1_of[i] = softmax(i, scores(i, S_BANKS[i % 2]))
+            if step == 0:
+                transpose_v1()
+            if 0 <= i + 2 < NB:
+                a1T_of[i + 2] = transposed(i + 2, a1_of[i + 2])
+            if 0 <= i + 3 < NB:
+                if i + 3 == CHUNK_BLOCKS - 1:
+                    y = start_chunk(0)
+                mix(i + 3, a1T_of[i + 3], y)
+                if (i + 3) % CHUNK_BLOCKS == 0:
+                    finish_chunk((i + 3) // CHUNK_BLOCKS, y)

@@ -22,14 +22,17 @@ BANK_BYTES = 4 * BANK
 BANKS = 8
 CHUNKS = T // BANK
 CHUNK_BLOCKS = BANK // P
+PIECES = N // BANK
 PIECE_COLS = BANK // 16
 SCALE = 0.1953125
-WARM_UP_MATMULS = 16
 MASKED = -1.0e30
+WARM_UP_MATMULS = 16
 
-Y_BANK = 0
 T_BANKS = (2, 3)
 S_BANKS = ((6, 7), (4, 5))
+NARROW_S_BANKS = (4, 5)
+Y_BANK = (6, 0)
+NOT_Y_BANKS = (2, 3, 4, 5, 6, 7)
 
 CAUSAL_PAIRS = T * (T + 1) // 2
 FLOPS = 2 * (2 * T * T * T + T * CAUSAL_PAIRS + B * P * CAUSAL_PAIRS + 2 * P * P * N)
@@ -88,7 +91,6 @@ def tile_inductionheadattentionsmaller_b_kernel(tc, table, pos, wq1, wk1, wv1, w
         nc.gpsimd.iota(u_minus_t[:], pattern=[[1, P]], base=0, channel_multiplier=-1)
         above_diag = held.tile([P, P], BF16, name="above_diag")
         nc.vector.tensor_scalar(above_diag[:], u_minus_t[:], 0.0, MASKED, op0=IS_GT, op1=MULT)
-
         not_row0 = held.tile([P, 1], F32, name="not_row0")
         nc.vector.memset(not_row0[:], 1.0)
         nc.vector.memset(not_row0[0:1, :], 0.0)
@@ -113,23 +115,23 @@ def tile_inductionheadattentionsmaller_b_kernel(tc, table, pos, wq1, wk1, wv1, w
             for a in range(NB):
                 copy_out(a, proj_sb[a][c][:], accs[a][:])
 
-        def project_in_turn(w_sb, proj_sb, c, banks):
+        def project_in_turn(w_sb, proj_sb, c):
             for a in range(NB):
-                acc = bank_f32(banks[a % len(banks)])
+                acc = bank_f32(a)
                 for f in range(NB):
                     project_step(acc, w_sb, a, c, f)
                 copy_out(a, proj_sb[a][c][:], acc[:])
 
         project_together(wk_sb, k_sb, 0)
-        project_in_turn(wk_sb, k_sb, 1, range(BANKS))
-        project_in_turn(wq_sb, q_sb, 1, range(BANKS))
-        project_in_turn(wq_sb, q_sb, 0, range(BANKS))
+        project_in_turn(wk_sb, k_sb, 1)
+        project_in_turn(wq_sb, q_sb, 1)
+        project_in_turn(wq_sb, q_sb, 0)
 
         def looked_up(piece):
             return table_sb[:].indirect(offsets[:, piece * PIECE_COLS : (piece + 1) * PIECE_COLS])
 
         def start_chunk(c):
-            y = psum.tile([P, B, BANK], F32, name="y", offset=Y_BANK * BANK_BYTES)
+            y = psum.tile([P, B, BANK], F32, name=f"y_chunk{c}", offset=Y_BANK[c] * BANK_BYTES)
             for s in range(B):
                 nc.tensor.matmul(y[:, s, :], lhsT=ident[:], rhs=looked_up(s * CHUNKS + c), start=True, stop=False)
             return y
@@ -142,13 +144,13 @@ def tile_inductionheadattentionsmaller_b_kernel(tc, table, pos, wq1, wk1, wv1, w
                 queue.dma_start(out[0:P, s * T + c * BANK : s * T + (c + 1) * BANK], y_sb[:])
 
         v1_sb = held.tile([P, N], BF16, name="v1_sb")
-        for piece in range(N // BANK):
-            v1_ps = bank_f32(2 + piece)
+        for piece in range(PIECES):
+            v1_ps = bank_f32(NOT_Y_BANKS[piece])
             nc.tensor.matmul(v1_ps[:], lhsT=wv1_sb[:], rhs=looked_up(piece), start=True, stop=True)
             copy_out(piece, v1_sb[:, piece * BANK : (piece + 1) * BANK], v1_ps[:])
         y = start_chunk(CHUNKS - 1)
-        for piece in range(N // BANK):
-            v2_ps = bank_f32(2 + (N // BANK + piece) % 6)
+        for piece in range(PIECES):
+            v2_ps = bank_f32(NOT_Y_BANKS[(PIECES + piece) % len(NOT_Y_BANKS)])
             nc.tensor.matmul(v2_ps[:], lhsT=wv2_sb[:], rhs=looked_up(piece), start=True, stop=True)
             v2_sb = staging.tile([P, BANK], F32, name="staged")
             copy_out(piece, v2_sb[:], v2_ps[:])
@@ -248,16 +250,20 @@ def tile_inductionheadattentionsmaller_b_kernel(tc, table, pos, wq1, wk1, wv1, w
         a1_of = {}
         a1T_of = {}
         for step in range(NB + 3):
-            i = NB - 1 - step
-            if 0 <= i:
-                a1_of[i] = softmax(i, scores(i, S_BANKS[i % 2]))
+            scored = NB - 1 - step
+            flipped = scored + 2
+            mixed = scored + 3
+            if CHUNK_BLOCKS <= scored:
+                a1_of[scored] = softmax(scored, scores(scored, S_BANKS[scored % 2]))
+            elif 0 <= scored:
+                a1_of[scored] = softmax(scored, scores(scored, NARROW_S_BANKS[scored % 2 : scored % 2 + 1]))
             if step == 0:
                 transpose_v1()
-            if 0 <= i + 2 < NB:
-                a1T_of[i + 2] = transposed(i + 2, a1_of[i + 2])
-            if 0 <= i + 3 < NB:
-                if i + 3 == CHUNK_BLOCKS - 1:
+            if 0 <= flipped < NB:
+                a1T_of[flipped] = transposed(flipped, a1_of[flipped])
+            if 0 <= mixed < NB:
+                if mixed == CHUNK_BLOCKS - 1:
                     y = start_chunk(0)
-                mix(i + 3, a1T_of[i + 3], y)
-                if (i + 3) % CHUNK_BLOCKS == 0:
-                    finish_chunk((i + 3) // CHUNK_BLOCKS, y)
+                mix(mixed, a1T_of[mixed], y)
+                if mixed % CHUNK_BLOCKS == 0:
+                    finish_chunk(mixed // CHUNK_BLOCKS, y)

@@ -158,20 +158,26 @@ def tile_inductionheadattentionsmaller_b_kernel(tc, table, pos, wq1, wk1, wv1, w
 
         v1T = held.tile([P, B * NB, P], BF16, name="v1T")
 
-        def transpose_v1():
-            for s in range(B):
-                v1T_ps = bank_bf16(T_BANKS[s])
-                for k in range(NB):
-                    j = (s * NB + k) * P
-                    nc.tensor.transpose(v1T_ps[:, k * P : (k + 1) * P], v1_sb[:, j : j + P], ident[:])
-                copy_out(s, v1T[:, s * NB : (s + 1) * NB, :], v1T_ps[:].rearrange("p (k m) -> p k m", m=P))
+        def v1_flips():
+            v1T_ps = [bank_bf16(T_BANKS[s]) for s in range(B)]
+            flips = [
+                (v1T_ps[s][:, k * P : (k + 1) * P], v1_sb[:, (s * NB + k) * P : (s * NB + k + 1) * P])
+                for s in range(B)
+                for k in range(NB)
+            ]
+            return v1T_ps, flips
 
-        def scores(i, banks):
+        def copy_v1T(v1T_ps):
+            for s in range(B):
+                copy_out(s, v1T[:, s * NB : (s + 1) * NB, :], v1T_ps[s][:].rearrange("p (k m) -> p k m", m=P))
+
+        def scores(i, banks, flips):
             width = (i + 1) * P
             col = (i % CHUNK_BLOCKS) * P
+            bounds = [(lo, min(lo + BANK, width)) for lo in range(0, width, BANK)]
+            first_woven = len(bounds) * NB - len(flips)
             pieces = []
-            for p, lo in enumerate(range(0, width, BANK)):
-                hi = min(lo + BANK, width)
+            for p, (lo, hi) in enumerate(bounds):
                 has_diagonal = hi == width
                 s_ps = bank_f32(banks[p])
                 for a in range(NB):
@@ -182,6 +188,9 @@ def tile_inductionheadattentionsmaller_b_kernel(tc, table, pos, wq1, wk1, wv1, w
                         start=(a == 0),
                         stop=(a == NB - 1 and not has_diagonal),
                     )
+                    if p * NB + a >= first_woven:
+                        to, frm = flips[p * NB + a - first_woven]
+                        nc.tensor.transpose(to, frm, ident[:])
                 if has_diagonal:
                     nc.tensor.matmul(
                         s_ps[:, hi - lo - P : hi - lo], lhsT=ident[:], rhs=above_diag[:], start=False, stop=True
@@ -225,11 +234,13 @@ def tile_inductionheadattentionsmaller_b_kernel(tc, table, pos, wq1, wk1, wv1, w
                 nc.vector.tensor_scalar_mul(a1[:, :width], expd[:, :width], inv_sum[:])
             return a1
 
-        def transposed(i, a1):
-            width = (i + 1) * P
+        def a1_flips(i, a1):
             a1T_ps = bank_bf16(T_BANKS[i % 2])
-            for k in range(i + 1):
-                nc.tensor.transpose(a1T_ps[:, k * P : (k + 1) * P], a1[:, k * P : (k + 1) * P], ident[:])
+            flips = [(a1T_ps[:, k * P : (k + 1) * P], a1[:, k * P : (k + 1) * P]) for k in range(i + 1)]
+            return a1T_ps, flips
+
+        def copy_a1T(i, a1T_ps):
+            width = (i + 1) * P
             a1T = work.tile([P, T], BF16, name="a1T")
             nc.scalar.copy(a1T[:, :width], a1T_ps[:, :width])
             return a1T
@@ -253,14 +264,24 @@ def tile_inductionheadattentionsmaller_b_kernel(tc, table, pos, wq1, wk1, wv1, w
             scored = NB - 1 - step
             flipped = scored + 2
             mixed = scored + 3
-            if CHUNK_BLOCKS <= scored:
-                a1_of[scored] = softmax(scored, scores(scored, S_BANKS[scored % 2]))
-            elif 0 <= scored:
-                a1_of[scored] = softmax(scored, scores(scored, NARROW_S_BANKS[scored % 2 : scored % 2 + 1]))
-            if step == 0:
-                transpose_v1()
+            flips = []
+            if step == 1:
+                v1T_ps, flips = v1_flips()
             if 0 <= flipped < NB:
-                a1T_of[flipped] = transposed(flipped, a1_of[flipped])
+                a1T_ps, flips = a1_flips(flipped, a1_of[flipped])
+            if CHUNK_BLOCKS <= scored:
+                pieces = scores(scored, S_BANKS[scored % 2], flips)
+            elif 0 <= scored:
+                pieces = scores(scored, NARROW_S_BANKS[scored % 2 : scored % 2 + 1], flips)
+            else:
+                for to, frm in flips:
+                    nc.tensor.transpose(to, frm, ident[:])
+            if step == 1:
+                copy_v1T(v1T_ps)
+            if 0 <= flipped < NB:
+                a1T_of[flipped] = copy_a1T(flipped, a1T_ps)
+            if 0 <= scored:
+                a1_of[scored] = softmax(scored, pieces)
             if 0 <= mixed < NB:
                 if mixed == CHUNK_BLOCKS - 1:
                     y = start_chunk(0)

@@ -8,6 +8,7 @@ I32 = mybir.dt.int32
 EXP = mybir.ActivationFunctionType.Exp
 IS_GT = mybir.AluOpType.is_gt
 MULT = mybir.AluOpType.mult
+ADD = mybir.AluOpType.add
 MAX = mybir.AluOpType.max
 X = mybir.AxisListType.X
 
@@ -31,8 +32,8 @@ WARM_UP_MATMULS = 16
 T_BANKS = (2, 3)
 S_BANKS = ((6, 7), (4, 5))
 NARROW_S_BANKS = (4, 5)
-Y_BANK = (6, 0)
-NOT_Y_BANKS = (2, 3, 4, 5, 6, 7)
+Y_BANKS = (0, 1)
+V2_BANKS = (6, 7, 5, 4)
 
 CAUSAL_PAIRS = T * (T + 1) // 2
 FLOPS = 2 * (2 * T * T * T + T * CAUSAL_PAIRS + B * P * CAUSAL_PAIRS + 2 * P * P * N)
@@ -130,31 +131,18 @@ def tile_inductionheadattentionsmaller_b_kernel(tc, table, pos, wq1, wk1, wv1, w
         def looked_up(piece):
             return table_sb[:].indirect(offsets[:, piece * PIECE_COLS : (piece + 1) * PIECE_COLS])
 
-        def start_chunk(c):
-            y = psum.tile([P, B, BANK], F32, name=f"y_chunk{c}", offset=Y_BANK[c] * BANK_BYTES)
-            for s in range(B):
-                nc.tensor.matmul(y[:, s, :], lhsT=ident[:], rhs=looked_up(s * CHUNKS + c), start=True, stop=False)
-            return y
-
-        def finish_chunk(c, y):
-            for s in range(B):
-                y_sb = staging.tile([P, BANK], F32, name="staged")
-                copy_out(s, y_sb[:], y[:, s, :])
-                queue = nc.sync if s % 2 == 0 else nc.scalar
-                queue.dma_start(out[0:P, s * T + c * BANK : s * T + (c + 1) * BANK], y_sb[:])
-
         v1_sb = held.tile([P, N], BF16, name="v1_sb")
         for piece in range(PIECES):
-            v1_ps = bank_f32(NOT_Y_BANKS[piece])
+            v1_ps = bank_f32(piece)
             nc.tensor.matmul(v1_ps[:], lhsT=wv1_sb[:], rhs=looked_up(piece), start=True, stop=True)
             copy_out(piece, v1_sb[:, piece * BANK : (piece + 1) * BANK], v1_ps[:])
-        y = start_chunk(CHUNKS - 1)
+        e_sb = held.tile([P, N], BF16, name="e_sb")
         for piece in range(PIECES):
-            v2_ps = bank_f32(NOT_Y_BANKS[(PIECES + piece) % len(NOT_Y_BANKS)])
-            nc.tensor.matmul(v2_ps[:], lhsT=wv2_sb[:], rhs=looked_up(piece), start=True, stop=True)
-            v2_sb = staging.tile([P, BANK], F32, name="staged")
-            copy_out(piece, v2_sb[:], v2_ps[:])
-            nc.sync.dma_start(out[P : 2 * P, piece * BANK : (piece + 1) * BANK], v2_sb[:])
+            e_ps = bank_f32(PIECES + piece)
+            nc.tensor.matmul(e_ps[:], lhsT=ident[:], rhs=looked_up(piece), start=True, stop=True)
+            copy_out(piece, e_sb[:, piece * BANK : (piece + 1) * BANK], e_ps[:])
+        e_by_seq = e_sb[:].rearrange("p (s t) -> p s t", s=B)
+        out_by_seq = out[0:P, :].rearrange("p (s t) -> p s t", s=B)
 
         v1T = held.tile([P, B * NB, P], BF16, name="v1T")
 
@@ -245,46 +233,58 @@ def tile_inductionheadattentionsmaller_b_kernel(tc, table, pos, wq1, wk1, wv1, w
             nc.scalar.copy(a1T[:, :width], a1T_ps[:, :width])
             return a1T
 
-        def mix(i, a1T, y):
-            col = (i % CHUNK_BLOCKS) * P
-            last_block = i % CHUNK_BLOCKS == 0
+        def mix(i, a1T):
+            b = Y_BANKS[i % 2]
+            y = psum.tile([P, B, P], F32, name=f"y_bank{b}", offset=b * BANK_BYTES)
             for s in range(B):
                 for k in range(i + 1):
                     nc.tensor.matmul(
-                        y[:, s, col : col + P],
+                        y[:, s, :],
                         lhsT=v1T[:, s * NB + k, :],
                         rhs=a1T[:, k * P : (k + 1) * P],
-                        start=False,
-                        stop=(last_block and k == i),
+                        start=(k == 0),
+                        stop=(k == i),
                     )
+            summed = staging.tile([P, B, P], F32, name="summed")
+            nc.vector.tensor_tensor(out=summed[:], in0=y[:], in1=e_by_seq[:, :, i * P : (i + 1) * P], op=ADD)
+            nc.sync.dma_start(out_by_seq[:, :, i * P : (i + 1) * P], summed[:])
+
+        def project_v2():
+            for piece in range(PIECES):
+                v2_ps = bank_f32(V2_BANKS[piece])
+                nc.tensor.matmul(v2_ps[:], lhsT=wv2_sb[:], rhs=looked_up(piece), start=True, stop=True)
+                v2_sb = staging.tile([P, BANK], F32, name="staged")
+                copy_out(1 if piece < PIECES // 2 else 0, v2_sb[:], v2_ps[:])
+                nc.sync.dma_start(out[P : 2 * P, piece * BANK : (piece + 1) * BANK], v2_sb[:])
 
         a1_of = {}
         a1T_of = {}
-        for step in range(NB + 3):
+        for step in range(NB):
             scored = NB - 1 - step
             flipped = scored + 2
             mixed = scored + 3
             flips = []
             if step == 1:
                 v1T_ps, flips = v1_flips()
-            if 0 <= flipped < NB:
+            if flipped < NB:
                 a1T_ps, flips = a1_flips(flipped, a1_of[flipped])
             if CHUNK_BLOCKS <= scored:
                 pieces = scores(scored, S_BANKS[scored % 2], flips)
-            elif 0 <= scored:
-                pieces = scores(scored, NARROW_S_BANKS[scored % 2 : scored % 2 + 1], flips)
             else:
-                for to, frm in flips:
-                    nc.tensor.transpose(to, frm, ident[:])
+                pieces = scores(scored, NARROW_S_BANKS[scored % 2 : scored % 2 + 1], flips)
             if step == 1:
                 copy_v1T(v1T_ps)
-            if 0 <= flipped < NB:
+            if flipped < NB:
                 a1T_of[flipped] = copy_a1T(flipped, a1T_ps)
-            if 0 <= scored:
-                a1_of[scored] = softmax(scored, pieces)
-            if 0 <= mixed < NB:
-                if mixed == CHUNK_BLOCKS - 1:
-                    y = start_chunk(0)
-                mix(mixed, a1T_of[mixed], y)
-                if mixed % CHUNK_BLOCKS == 0:
-                    finish_chunk(mixed // CHUNK_BLOCKS, y)
+            a1_of[scored] = softmax(scored, pieces)
+            if mixed < NB:
+                mix(mixed, a1T_of[mixed])
+
+        project_v2()
+        for i in (1, 0):
+            a1T_ps, flips = a1_flips(i, a1_of[i])
+            for to, frm in flips:
+                nc.tensor.transpose(to, frm, ident[:])
+            a1T_of[i] = copy_a1T(i, a1T_ps)
+        for i in (2, 1, 0):
+            mix(i, a1T_of[i])

@@ -34,6 +34,7 @@ S_BANKS = ((6, 7), (4, 5))
 NARROW_S_BANKS = (4, 5)
 Y_BANKS = (0, 1)
 V2_BANKS = (6, 7, 5, 4)
+LAST_Y_BANK = V2_BANKS[0]
 
 CAUSAL_PAIRS = T * (T + 1) // 2
 FLOPS = 2 * (2 * T * T * T + T * CAUSAL_PAIRS + B * P * CAUSAL_PAIRS + 2 * P * P * N)
@@ -71,9 +72,13 @@ def tile_inductionheadattentionsmaller_b_kernel(tc, table, pos, wq1, wk1, wv1, w
         pos_sb = [held.tile([P, T], BF16, name=f"pos_sb{f}") for f in range(NB)]
         wk_sb = [held.tile([P, T], BF16, name=f"wk_sb{f}") for f in range(NB)]
         wq_sb = [held.tile([P, T], BF16, name=f"wq_sb{f}") for f in range(NB)]
-        for f in range(NB):
-            nc.sync.dma_start(pos_sb[f][:], pos[f * P : (f + 1) * P, :])
+        for c in range(CHUNKS):
+            nc.scalar.dma_start(wk_sb[0][:, c * BANK : (c + 1) * BANK], wk1[0:P, c * BANK : (c + 1) * BANK])
+        for f in range(1, NB):
             nc.scalar.dma_start(wk_sb[f][:], wk1[f * P : (f + 1) * P, :])
+        for c in range(CHUNKS):
+            for f in range(NB):
+                nc.sync.dma_start(pos_sb[f][:, c * BANK : (c + 1) * BANK], pos[f * P : (f + 1) * P, c * BANK : (c + 1) * BANK])
         for f in range(NB):
             queue = nc.sync if f % 2 == 0 else nc.scalar
             queue.dma_start(wq_sb[f][:], wq1[f * P : (f + 1) * P, :])
@@ -234,7 +239,7 @@ def tile_inductionheadattentionsmaller_b_kernel(tc, table, pos, wq1, wk1, wv1, w
             return a1T
 
         def mix(i, a1T):
-            b = Y_BANKS[i % 2]
+            b = Y_BANKS[i % 2] if i > 0 else LAST_Y_BANK
             y = psum.tile([P, B, P], F32, name=f"y_bank{b}", offset=b * BANK_BYTES)
             for s in range(B):
                 for k in range(i + 1):
@@ -249,10 +254,14 @@ def tile_inductionheadattentionsmaller_b_kernel(tc, table, pos, wq1, wk1, wv1, w
             nc.vector.tensor_tensor(out=summed[:], in0=y[:], in1=e_by_seq[:, :, i * P : (i + 1) * P], op=ADD)
             nc.sync.dma_start(out_by_seq[:, :, i * P : (i + 1) * P], summed[:])
 
-        def project_v2():
+        def project_v2(flips):
+            first_woven = PIECES - len(flips)
             for piece in range(PIECES):
                 v2_ps = bank_f32(V2_BANKS[piece])
                 nc.tensor.matmul(v2_ps[:], lhsT=wv2_sb[:], rhs=looked_up(piece), start=True, stop=True)
+                if piece >= first_woven:
+                    to, frm = flips[piece - first_woven]
+                    nc.tensor.transpose(to, frm, ident[:])
                 v2_sb = staging.tile([P, BANK], F32, name="staged")
                 copy_out(1 if piece < PIECES // 2 else 0, v2_sb[:], v2_ps[:])
                 nc.sync.dma_start(out[P : 2 * P, piece * BANK : (piece + 1) * BANK], v2_sb[:])
@@ -280,11 +289,13 @@ def tile_inductionheadattentionsmaller_b_kernel(tc, table, pos, wq1, wk1, wv1, w
             if mixed < NB:
                 mix(mixed, a1T_of[mixed])
 
-        project_v2()
+        a1T_ps_of = {}
+        flips = []
         for i in (1, 0):
-            a1T_ps, flips = a1_flips(i, a1_of[i])
-            for to, frm in flips:
-                nc.tensor.transpose(to, frm, ident[:])
-            a1T_of[i] = copy_a1T(i, a1T_ps)
+            a1T_ps_of[i], flips_of_block = a1_flips(i, a1_of[i])
+            flips.extend(flips_of_block)
+        project_v2(flips)
+        for i in (1, 0):
+            a1T_of[i] = copy_a1T(i, a1T_ps_of[i])
         for i in (2, 1, 0):
             mix(i, a1T_of[i])

@@ -221,10 +221,8 @@ def tile_inductionheadattentionsmaller_b_kernel(tc, table, pos, wq1, wk1, wv1, w
             else:
                 nc.vector.reciprocal(inv_sum[:], piece_sum[:, 0:1])
             a1 = work.tile([P, T], BF16, name="a1")
-            if i == 0:
-                nc.vector.tensor_scalar(a1[:, :width], expd[:, :width], inv_sum[:], not_row0[:], op0=MULT, op1=MULT)
-            else:
-                nc.vector.tensor_scalar_mul(a1[:, :width], expd[:, :width], inv_sum[:])
+            row_gate = not_row0[:] if i == 0 else 1.0
+            nc.gpsimd.tensor_scalar(a1[:, :width], expd[:, :width], inv_sum[:], row_gate, op0=MULT, op1=MULT)
             return a1
 
         def a1_flips(i, a1):

@@ -30,11 +30,12 @@ MASKED = -1.0e30
 WARM_UP_MATMULS = 16
 
 T_BANKS = (2, 3)
-S_BANKS = ((6, 7), (4, 5))
+FILL_BANKS = (0, 1)
 NARROW_S_BANKS = (4, 5)
-Y_BANKS = (0, 1)
-V2_BANKS = (6, 7, 5, 4)
-LAST_Y_BANK = V2_BANKS[0]
+CHUNK_Y_BANKS = (6, 7)
+WIDE_S_BANKS = ((4, 5), (6, 7))
+V2_BANKS = (6, 7, 1, 0)
+Y_BANKS = {7: (0,), 6: (6,), 5: (7,), 4: (4, 5)}
 
 CAUSAL_PAIRS = T * (T + 1) // 2
 FLOPS = 2 * (2 * T * T * T + T * CAUSAL_PAIRS + B * P * CAUSAL_PAIRS + 2 * P * P * N)
@@ -72,13 +73,16 @@ def tile_inductionheadattentionsmaller_b_kernel(tc, table, pos, wq1, wk1, wv1, w
         pos_sb = [held.tile([P, T], BF16, name=f"pos_sb{f}") for f in range(NB)]
         wk_sb = [held.tile([P, T], BF16, name=f"wk_sb{f}") for f in range(NB)]
         wq_sb = [held.tile([P, T], BF16, name=f"wq_sb{f}") for f in range(NB)]
+
+        def load_pos_chunk(c):
+            for f in range(NB):
+                nc.sync.dma_start(pos_sb[f][:, c * BANK : (c + 1) * BANK], pos[f * P : (f + 1) * P, c * BANK : (c + 1) * BANK])
+
         for c in range(CHUNKS):
             nc.scalar.dma_start(wk_sb[0][:, c * BANK : (c + 1) * BANK], wk1[0:P, c * BANK : (c + 1) * BANK])
         for f in range(1, NB):
             nc.scalar.dma_start(wk_sb[f][:], wk1[f * P : (f + 1) * P, :])
-        for c in range(CHUNKS):
-            for f in range(NB):
-                nc.sync.dma_start(pos_sb[f][:, c * BANK : (c + 1) * BANK], pos[f * P : (f + 1) * P, c * BANK : (c + 1) * BANK])
+        load_pos_chunk(0)
         for f in range(NB):
             queue = nc.sync if f % 2 == 0 else nc.scalar
             queue.dma_start(wq_sb[f][:], wq1[f * P : (f + 1) * P, :])
@@ -90,12 +94,13 @@ def tile_inductionheadattentionsmaller_b_kernel(tc, table, pos, wq1, wk1, wv1, w
         nc.scalar.dma_start(wv1_sb[:], wv1)
         wv2_sb = held.tile([P, P], BF16, name="wv2_sb")
         nc.scalar.dma_start(wv2_sb[:], wv2)
+        load_pos_chunk(1)
 
         ident = held.tile([P, P], BF16, name="ident")
         make_identity(nc, ident[:])
-        u_minus_t = held.tile([P, P], I32, name="u_minus_t")
-        nc.gpsimd.iota(u_minus_t[:], pattern=[[1, P]], base=0, channel_multiplier=-1)
-        above_diag = held.tile([P, P], BF16, name="above_diag")
+        u_minus_t = held.tile([P, BANK], I32, name="u_minus_t")
+        nc.gpsimd.iota(u_minus_t[:], pattern=[[1, BANK]], base=P - BANK, channel_multiplier=-1)
+        above_diag = held.tile([P, BANK], BF16, name="above_diag")
         nc.vector.tensor_scalar(above_diag[:], u_minus_t[:], 0.0, MASKED, op0=IS_GT, op1=MULT)
         not_row0 = held.tile([P, 1], F32, name="not_row0")
         nc.vector.memset(not_row0[:], 1.0)
@@ -121,17 +126,23 @@ def tile_inductionheadattentionsmaller_b_kernel(tc, table, pos, wq1, wk1, wv1, w
             for a in range(NB):
                 copy_out(a, proj_sb[a][c][:], accs[a][:])
 
-        def project_in_turn(w_sb, proj_sb, c):
-            for a in range(NB):
-                acc = bank_f32(a)
-                for f in range(NB):
-                    project_step(acc, w_sb, a, c, f)
-                copy_out(a, proj_sb[a][c][:], acc[:])
+        flips = []
+
+        def weave():
+            if flips:
+                to, frm = flips.pop(0)
+                nc.tensor.transpose(to, frm, ident[:])
+
+        def project_row_block(w_sb, proj_sb, c, a, bank):
+            acc = bank_f32(bank)
+            for f in range(NB):
+                project_step(acc, w_sb, a, c, f)
+                weave()
+            copy_out(a, proj_sb[a][c][:], acc[:])
 
         project_together(wk_sb, k_sb, 0)
-        project_in_turn(wk_sb, k_sb, 1)
-        project_in_turn(wq_sb, q_sb, 1)
-        project_in_turn(wq_sb, q_sb, 0)
+        for a in range(NB):
+            project_row_block(wq_sb, q_sb, 0, a, a)
 
         def looked_up(piece):
             return table_sb[:].indirect(offsets[:, piece * PIECE_COLS : (piece + 1) * PIECE_COLS])
@@ -146,32 +157,27 @@ def tile_inductionheadattentionsmaller_b_kernel(tc, table, pos, wq1, wk1, wv1, w
             e_ps = bank_f32(PIECES + piece)
             nc.tensor.matmul(e_ps[:], lhsT=ident[:], rhs=looked_up(piece), start=True, stop=True)
             copy_out(piece, e_sb[:, piece * BANK : (piece + 1) * BANK], e_ps[:])
-        e_by_seq = e_sb[:].rearrange("p (s t) -> p s t", s=B)
-        out_by_seq = out[0:P, :].rearrange("p (s t) -> p s t", s=B)
 
         v1T = held.tile([P, B * NB, P], BF16, name="v1T")
 
         def v1_flips():
             v1T_ps = [bank_bf16(T_BANKS[s]) for s in range(B)]
-            flips = [
-                (v1T_ps[s][:, k * P : (k + 1) * P], v1_sb[:, (s * NB + k) * P : (s * NB + k + 1) * P])
-                for s in range(B)
-                for k in range(NB)
-            ]
-            return v1T_ps, flips
+            for s in range(B):
+                for k in range(NB):
+                    flips.append((v1T_ps[s][:, k * P : (k + 1) * P], v1_sb[:, (s * NB + k) * P : (s * NB + k + 1) * P]))
+            return v1T_ps
 
         def copy_v1T(v1T_ps):
             for s in range(B):
                 copy_out(s, v1T[:, s * NB : (s + 1) * NB, :], v1T_ps[s][:].rearrange("p (k m) -> p k m", m=P))
 
-        def scores(i, banks, flips):
+        def scores(i, banks):
             width = (i + 1) * P
             col = (i % CHUNK_BLOCKS) * P
             bounds = [(lo, min(lo + BANK, width)) for lo in range(0, width, BANK)]
             first_woven = len(bounds) * NB - len(flips)
             pieces = []
             for p, (lo, hi) in enumerate(bounds):
-                has_diagonal = hi == width
                 s_ps = bank_f32(banks[p])
                 for a in range(NB):
                     nc.tensor.matmul(
@@ -179,24 +185,23 @@ def tile_inductionheadattentionsmaller_b_kernel(tc, table, pos, wq1, wk1, wv1, w
                         lhsT=q_sb[a][i // CHUNK_BLOCKS][:, col : col + P],
                         rhs=k_sb[a][p][:, : hi - lo],
                         start=(a == 0),
-                        stop=(a == NB - 1 and not has_diagonal),
+                        stop=(a == NB - 1),
                     )
                     if p * NB + a >= first_woven:
-                        to, frm = flips[p * NB + a - first_woven]
-                        nc.tensor.transpose(to, frm, ident[:])
-                if has_diagonal:
-                    nc.tensor.matmul(
-                        s_ps[:, hi - lo - P : hi - lo], lhsT=ident[:], rhs=above_diag[:], start=False, stop=True
-                    )
-                pieces.append((lo, hi, s_ps))
+                        weave()
+                pieces.append((lo, hi, s_ps[:, : hi - lo]))
             return pieces
 
         def softmax(i, pieces):
             width = (i + 1) * P
             two_pieces = len(pieces) == 2
             piece_max = stats.tile([P, CHUNKS], F32, name="piece_max")
-            for p, (lo, hi, s_ps) in enumerate(pieces):
-                nc.vector.reduce_max(out=piece_max[:, p : p + 1], in_=s_ps[:, : hi - lo], axis=X)
+            lo, hi, s = pieces[-1]
+            masked = work.tile([P, BANK], F32, name="masked")
+            nc.vector.tensor_tensor(out=masked[:, : hi - lo], in0=s, in1=above_diag[:, BANK - (hi - lo) :], op=ADD)
+            pieces = pieces[:-1] + [(lo, hi, masked[:, : hi - lo])]
+            for p, (lo, hi, s) in enumerate(pieces):
+                nc.vector.reduce_max(out=piece_max[:, p : p + 1], in_=s, axis=X)
             shift = stats.tile([P, 1], F32, name="shift")
             if two_pieces:
                 nc.vector.tensor_scalar(shift[:], piece_max[:, 0:1], piece_max[:, 1:2], -SCALE, op0=MAX, op1=MULT)
@@ -204,10 +209,10 @@ def tile_inductionheadattentionsmaller_b_kernel(tc, table, pos, wq1, wk1, wv1, w
                 nc.vector.tensor_scalar_mul(shift[:], piece_max[:, 0:1], -SCALE)
             expd = work.tile([P, T], F32, name="expd")
             piece_sum = stats.tile([P, CHUNKS], F32, name="piece_sum")
-            for p, (lo, hi, s_ps) in enumerate(pieces):
+            for p, (lo, hi, s) in enumerate(pieces):
                 nc.scalar.activation(
                     out=expd[:, lo:hi],
-                    in_=s_ps[:, : hi - lo],
+                    in_=s,
                     func=EXP,
                     bias=shift[:],
                     scale=SCALE,
@@ -227,73 +232,109 @@ def tile_inductionheadattentionsmaller_b_kernel(tc, table, pos, wq1, wk1, wv1, w
 
         def a1_flips(i, a1):
             a1T_ps = bank_bf16(T_BANKS[i % 2])
-            flips = [(a1T_ps[:, k * P : (k + 1) * P], a1[:, k * P : (k + 1) * P]) for k in range(i + 1)]
-            return a1T_ps, flips
+            for k in range(i + 1):
+                flips.append((a1T_ps[:, k * P : (k + 1) * P], a1[:, k * P : (k + 1) * P]))
+            return a1T_ps[:, : (i + 1) * P].rearrange("p (k t) -> p k t", t=P)
+
+        fill = [(wk_sb, k_sb, a) for a in range(NB)] + [(wq_sb, q_sb, a) for a in range(NB)]
+
+        def fill_row_blocks(count):
+            for n in range(count):
+                w_sb, proj_sb, a = fill.pop(0)
+                project_row_block(w_sb, proj_sb, 1, a, FILL_BANKS[a % 2])
+
+        chunk_a1T = held.tile([P, CHUNK_BLOCKS, BANK], BF16, name="chunk_a1T")
+
+        def copy_chunk_a1T(i, a1T_ps):
+            nc.scalar.copy(chunk_a1T[:, : i + 1, i * P : (i + 1) * P], a1T_ps)
+
+        a1 = None
+        for i in range(CHUNK_BLOCKS - 1, -1, -1):
+            pieces = scores(i, NARROW_S_BANKS[i % 2 : i % 2 + 1])
+            if i == CHUNK_BLOCKS - 1:
+                v1T_ps = v1_flips()
+            else:
+                a1T_ps = a1_flips(i + 1, a1)
+            a1 = softmax(i, pieces)
+            fill_row_blocks(2)
+            if i == CHUNK_BLOCKS - 1:
+                copy_v1T(v1T_ps)
+            else:
+                copy_chunk_a1T(i + 1, a1T_ps)
+        a1T_ps = a1_flips(0, a1)
+        fill_row_blocks(2)
+        copy_chunk_a1T(0, a1T_ps)
+        fill_row_blocks(2)
+
+        for s in range(B):
+            y = bank_f32(CHUNK_Y_BANKS[s])
+            for k in range(CHUNK_BLOCKS):
+                nc.tensor.matmul(
+                    y[:, k * P :],
+                    lhsT=v1T[:, s * NB + k, :],
+                    rhs=chunk_a1T[:, k, k * P :],
+                    start=(k == 0),
+                    stop=(k == CHUNK_BLOCKS - 1),
+                )
+            summed = staging.tile([P, BANK], F32, name="summed")
+            nc.vector.tensor_tensor(out=summed[:], in0=y[:], in1=e_sb[:, s * T : s * T + BANK], op=ADD)
+            nc.sync.dma_start(out[0:P, s * T : s * T + BANK], summed[:])
+        fill_row_blocks(len(fill))
+
+        e_by_seq = e_sb[:].rearrange("p (s t) -> p s t", s=B)
+        out_by_seq = out[0:P, :].rearrange("p (s t) -> p s t", s=B)
 
         def copy_a1T(i, a1T_ps):
-            width = (i + 1) * P
-            a1T = work.tile([P, T], BF16, name="a1T")
-            nc.scalar.copy(a1T[:, :width], a1T_ps[:, :width])
+            a1T = work.tile([P, NB, P], BF16, name="a1T")
+            nc.scalar.copy(a1T[:, : i + 1, :], a1T_ps)
             return a1T
 
         def mix(i, a1T):
-            b = Y_BANKS[i % 2] if i > 0 else LAST_Y_BANK
-            y = psum.tile([P, B, P], F32, name=f"y_bank{b}", offset=b * BANK_BYTES)
-            for s in range(B):
-                for k in range(i + 1):
-                    nc.tensor.matmul(
-                        y[:, s, :],
-                        lhsT=v1T[:, s * NB + k, :],
-                        rhs=a1T[:, k * P : (k + 1) * P],
-                        start=(k == 0),
-                        stop=(k == i),
-                    )
-            summed = staging.tile([P, B, P], F32, name="summed")
-            nc.vector.tensor_tensor(out=summed[:], in0=y[:], in1=e_by_seq[:, :, i * P : (i + 1) * P], op=ADD)
-            nc.sync.dma_start(out_by_seq[:, :, i * P : (i + 1) * P], summed[:])
+            seqs_of_bank = B // len(Y_BANKS[i])
+            for n, bank in enumerate(Y_BANKS[i]):
+                y = psum.tile([P, seqs_of_bank, P], F32, name=f"y{seqs_of_bank}_bank{bank}", offset=bank * BANK_BYTES)
+                first = n * seqs_of_bank
+                for s in range(seqs_of_bank):
+                    for k in range(i + 1):
+                        nc.tensor.matmul(
+                            y[:, s, :],
+                            lhsT=v1T[:, (first + s) * NB + k, :],
+                            rhs=a1T[:, k, :],
+                            start=(k == 0),
+                            stop=(k == i),
+                        )
+                        weave()
+                summed = staging.tile([P, seqs_of_bank, P], F32, name=f"summed{seqs_of_bank}")
+                there = (slice(None), slice(first, first + seqs_of_bank), slice(i * P, (i + 1) * P))
+                nc.vector.tensor_tensor(out=summed[:], in0=y[:], in1=e_by_seq[there], op=ADD)
+                nc.sync.dma_start(out_by_seq[there], summed[:])
 
-        def project_v2(flips):
-            first_woven = PIECES - len(flips)
+        def project_v2():
             for piece in range(PIECES):
                 v2_ps = bank_f32(V2_BANKS[piece])
                 nc.tensor.matmul(v2_ps[:], lhsT=wv2_sb[:], rhs=looked_up(piece), start=True, stop=True)
-                if piece >= first_woven:
-                    to, frm = flips[piece - first_woven]
-                    nc.tensor.transpose(to, frm, ident[:])
+                weave()
+                weave()
                 v2_sb = staging.tile([P, BANK], F32, name="staged")
-                copy_out(1 if piece < PIECES // 2 else 0, v2_sb[:], v2_ps[:])
+                copy_out(piece, v2_sb[:], v2_ps[:])
                 nc.sync.dma_start(out[P : 2 * P, piece * BANK : (piece + 1) * BANK], v2_sb[:])
 
         a1_of = {}
         a1T_of = {}
-        for step in range(NB):
-            scored = NB - 1 - step
-            flipped = scored + 2
-            mixed = scored + 3
-            flips = []
-            if step == 1:
-                v1T_ps, flips = v1_flips()
-            if flipped < NB:
-                a1T_ps, flips = a1_flips(flipped, a1_of[flipped])
-            if CHUNK_BLOCKS <= scored:
-                pieces = scores(scored, S_BANKS[scored % 2], flips)
-            else:
-                pieces = scores(scored, NARROW_S_BANKS[scored % 2 : scored % 2 + 1], flips)
-            if step == 1:
-                copy_v1T(v1T_ps)
-            if flipped < NB:
-                a1T_of[flipped] = copy_a1T(flipped, a1T_ps)
-            a1_of[scored] = softmax(scored, pieces)
-            if mixed < NB:
-                mix(mixed, a1T_of[mixed])
+        for i in range(NB - 1, CHUNK_BLOCKS - 1, -1):
+            if i + 2 < NB:
+                a1T_ps = a1_flips(i + 2, a1_of[i + 2])
+            pieces = scores(i, WIDE_S_BANKS[i % 2])
+            if i + 2 < NB:
+                a1T_of[i + 2] = copy_a1T(i + 2, a1T_ps)
+            a1_of[i] = softmax(i, pieces)
 
-        a1T_ps_of = {}
-        flips = []
-        for i in (1, 0):
-            a1T_ps_of[i], flips_of_block = a1_flips(i, a1_of[i])
-            flips.extend(flips_of_block)
-        project_v2(flips)
-        for i in (1, 0):
-            a1T_of[i] = copy_a1T(i, a1T_ps_of[i])
-        for i in (2, 1, 0):
-            mix(i, a1T_of[i])
+        mix(7, a1T_of[7])
+        a1T_ps = a1_flips(5, a1_of[5])
+        project_v2()
+        a1T_of[5] = copy_a1T(5, a1T_ps)
+        a1T_ps = a1_flips(4, a1_of[4])
+        mix(6, a1T_of[6])
+        a1T_of[4] = copy_a1T(4, a1T_ps)
+        mix(5, a1T_of[5])
+        mix(4, a1T_of[4])

@@ -30,12 +30,12 @@ MASKED = -1.0e30
 WARM_UP_MATMULS = 16
 
 T_BANKS = (2, 3)
-FILL_BANKS = (0, 1)
+FILL_BANKS = (0, 1, 6, 7)
 NARROW_S_BANKS = (4, 5)
-CHUNK_Y_BANKS = (6, 7)
-WIDE_S_BANKS = ((4, 5), (6, 7))
-V2_BANKS = (6, 7, 1, 0)
-Y_BANKS = {7: (0,), 6: (6,), 5: (7,), 4: (4, 5)}
+WIDE_S_BANKS = ((6, 7), (4, 5))
+V2_BANKS = (4, 5, 0, 1)
+CHUNK_Y_BANKS = (1, 4)
+Y_BANKS = {7: (0,), 6: (5,), 5: (0,), 4: (6, 7)}
 
 CAUSAL_PAIRS = T * (T + 1) // 2
 FLOPS = 2 * (2 * T * T * T + T * CAUSAL_PAIRS + B * P * CAUSAL_PAIRS + 2 * P * P * N)
@@ -241,7 +241,7 @@ def tile_inductionheadattentionsmaller_b_kernel(tc, table, pos, wq1, wk1, wv1, w
         def fill_row_blocks(count):
             for n in range(count):
                 w_sb, proj_sb, a = fill.pop(0)
-                project_row_block(w_sb, proj_sb, 1, a, FILL_BANKS[a % 2])
+                project_row_block(w_sb, proj_sb, 1, a, FILL_BANKS[a % len(FILL_BANKS)])
 
         chunk_a1T = held.tile([P, CHUNK_BLOCKS, BANK], BF16, name="chunk_a1T")
 
@@ -264,21 +264,6 @@ def tile_inductionheadattentionsmaller_b_kernel(tc, table, pos, wq1, wk1, wv1, w
         a1T_ps = a1_flips(0, a1)
         fill_row_blocks(2)
         copy_chunk_a1T(0, a1T_ps)
-        fill_row_blocks(2)
-
-        for s in range(B):
-            y = bank_f32(CHUNK_Y_BANKS[s])
-            for k in range(CHUNK_BLOCKS):
-                nc.tensor.matmul(
-                    y[:, k * P :],
-                    lhsT=v1T[:, s * NB + k, :],
-                    rhs=chunk_a1T[:, k, k * P :],
-                    start=(k == 0),
-                    stop=(k == CHUNK_BLOCKS - 1),
-                )
-            summed = staging.tile([P, BANK], F32, name="summed")
-            nc.vector.tensor_tensor(out=summed[:], in0=y[:], in1=e_sb[:, s * T : s * T + BANK], op=ADD)
-            nc.sync.dma_start(out[0:P, s * T : s * T + BANK], summed[:])
         fill_row_blocks(len(fill))
 
         e_by_seq = e_sb[:].rearrange("p (s t) -> p s t", s=B)
@@ -290,6 +275,7 @@ def tile_inductionheadattentionsmaller_b_kernel(tc, table, pos, wq1, wk1, wv1, w
             return a1T
 
         def mix(i, a1T):
+            first_woven = B * (i + 1) - len(flips)
             seqs_of_bank = B // len(Y_BANKS[i])
             for n, bank in enumerate(Y_BANKS[i]):
                 y = psum.tile([P, seqs_of_bank, P], F32, name=f"y{seqs_of_bank}_bank{bank}", offset=bank * BANK_BYTES)
@@ -303,11 +289,26 @@ def tile_inductionheadattentionsmaller_b_kernel(tc, table, pos, wq1, wk1, wv1, w
                             start=(k == 0),
                             stop=(k == i),
                         )
-                        weave()
+                        if (first + s) * (i + 1) + k >= first_woven:
+                            weave()
                 summed = staging.tile([P, seqs_of_bank, P], F32, name=f"summed{seqs_of_bank}")
                 there = (slice(None), slice(first, first + seqs_of_bank), slice(i * P, (i + 1) * P))
                 nc.vector.tensor_tensor(out=summed[:], in0=y[:], in1=e_by_seq[there], op=ADD)
                 nc.sync.dma_start(out_by_seq[there], summed[:])
+
+        def mix_chunk(s):
+            y = bank_f32(CHUNK_Y_BANKS[s])
+            for k in range(CHUNK_BLOCKS):
+                nc.tensor.matmul(
+                    y[:, k * P :],
+                    lhsT=v1T[:, s * NB + k, :],
+                    rhs=chunk_a1T[:, k, k * P :],
+                    start=(k == 0),
+                    stop=(k == CHUNK_BLOCKS - 1),
+                )
+            summed = staging.tile([P, BANK], F32, name="summed_chunk")
+            nc.vector.tensor_tensor(out=summed[:], in0=y[:], in1=e_sb[:, s * T : s * T + BANK], op=ADD)
+            nc.sync.dma_start(out[0:P, s * T : s * T + BANK], summed[:])
 
         def project_v2():
             for piece in range(PIECES):
@@ -330,9 +331,11 @@ def tile_inductionheadattentionsmaller_b_kernel(tc, table, pos, wq1, wk1, wv1, w
             a1_of[i] = softmax(i, pieces)
 
         mix(7, a1T_of[7])
+        mix_chunk(0)
         a1T_ps = a1_flips(5, a1_of[5])
         project_v2()
         a1T_of[5] = copy_a1T(5, a1T_ps)
+        mix_chunk(1)
         a1T_ps = a1_flips(4, a1_of[4])
         mix(6, a1T_of[6])
         a1T_of[4] = copy_a1T(4, a1T_ps)

@@ -33,9 +33,9 @@ T_BANKS = (2, 3)
 FILL_BANKS = (0, 1, 6, 7)
 NARROW_S_BANKS = (4, 5)
 WIDE_S_BANKS = ((6, 7), (4, 5))
-V2_BANKS = (4, 5, 0, 1)
-CHUNK_Y_BANKS = (1, 4)
-Y_BANKS = {7: (0,), 6: (5,), 5: (0,), 4: (6, 7)}
+V2_BANKS = (4, 5, 1, 0)
+CHUNK_Y_BANKS = (4, 5)
+Y_BANKS = {7: (0,), 6: (1,), 5: (0,), 4: (6, 7)}
 
 CAUSAL_PAIRS = T * (T + 1) // 2
 FLOPS = 2 * (2 * T * T * T + T * CAUSAL_PAIRS + B * P * CAUSAL_PAIRS + 2 * P * P * N)
@@ -314,10 +314,11 @@ def tile_inductionheadattentionsmaller_b_kernel(tc, table, pos, wq1, wk1, wv1, w
             for piece in range(PIECES):
                 v2_ps = bank_f32(V2_BANKS[piece])
                 nc.tensor.matmul(v2_ps[:], lhsT=wv2_sb[:], rhs=looked_up(piece), start=True, stop=True)
-                weave()
-                weave()
+                if piece >= PIECES // 2:
+                    for n in range(3):
+                        weave()
                 v2_sb = staging.tile([P, BANK], F32, name="staged")
-                copy_out(piece, v2_sb[:], v2_ps[:])
+                copy_out(1 if piece < PIECES // 2 else 0, v2_sb[:], v2_ps[:])
                 nc.sync.dma_start(out[P : 2 * P, piece * BANK : (piece + 1) * BANK], v2_sb[:])
 
         a1_of = {}
@@ -331,10 +332,10 @@ def tile_inductionheadattentionsmaller_b_kernel(tc, table, pos, wq1, wk1, wv1, w
             a1_of[i] = softmax(i, pieces)
 
         mix(7, a1T_of[7])
-        mix_chunk(0)
         a1T_ps = a1_flips(5, a1_of[5])
         project_v2()
         a1T_of[5] = copy_a1T(5, a1T_ps)
+        mix_chunk(0)
         mix_chunk(1)
         a1T_ps = a1_flips(4, a1_of[4])
         mix(6, a1T_of[6])

@@ -27,7 +27,7 @@ PIECES = N // BANK
 PIECE_COLS = BANK // 16
 SCALE = 0.1953125
 MASKED = -1.0e30
-WARM_UP_MATMULS = 16
+WARM_UP_MATMULS = 12
 
 T_BANKS = (2, 3)
 FILL_BANKS = (0, 1, 6, 7)

@@ -6,6 +6,7 @@ F32 = mybir.dt.float32
 U16 = mybir.dt.uint16
 I32 = mybir.dt.int32
 EXP = mybir.ActivationFunctionType.Exp
+COPY = mybir.ActivationFunctionType.Copy
 IS_GT = mybir.AluOpType.is_gt
 MULT = mybir.AluOpType.mult
 ADD = mybir.AluOpType.add
@@ -227,7 +228,10 @@ def tile_inductionheadattentionsmaller_b_kernel(tc, table, pos, wq1, wk1, wv1, w
                 nc.vector.reciprocal(inv_sum[:], piece_sum[:, 0:1])
             a1 = work.tile([P, T], BF16, name="a1")
             row_gate = not_row0[:] if i == 0 else 1.0
-            nc.gpsimd.tensor_scalar(a1[:, :width], expd[:, :width], inv_sum[:], row_gate, op0=MULT, op1=MULT)
+            head = pieces[0][1]
+            nc.gpsimd.tensor_scalar(a1[:, :head], expd[:, :head], inv_sum[:], row_gate, op0=MULT, op1=MULT)
+            if two_pieces:
+                nc.scalar.activation(out=a1[:, head:width], in_=expd[:, head:width], func=COPY, scale=inv_sum[:])
             return a1
 
         def a1_flips(i, a1):

import concourse.mybir as mybir
from concourse.masks import make_identity

BF16 = mybir.dt.bfloat16
F32 = mybir.dt.float32
U16 = mybir.dt.uint16
I32 = mybir.dt.int32
EXP = mybir.ActivationFunctionType.Exp
COPY = mybir.ActivationFunctionType.Copy
IS_GT = mybir.AluOpType.is_gt
MULT = mybir.AluOpType.mult
ADD = mybir.AluOpType.add
MAX = mybir.AluOpType.max
X = mybir.AxisListType.X

P = 128
V = 4096
T = 1024
B = 2
N = B * T
NB = T // P
BANK = 512
BANK_BYTES = 4 * BANK
BANKS = 8
CHUNKS = T // BANK
CHUNK_BLOCKS = BANK // P
PIECES = N // BANK
PIECE_COLS = BANK // 16
SCALE = 0.1953125
MASKED = -1.0e30
WARM_UP_MATMULS = 12

T_BANKS = (2, 3)
FILL_BANKS = (0, 1, 6, 7)
NARROW_S_BANKS = (4, 5)
WIDE_S_BANKS = ((6, 7), (4, 5))
V2_BANKS = (4, 5, 1, 0)
CHUNK_Y_BANKS = (4, 5)
Y_BANKS = {7: (0,), 6: (1,), 5: (0,), 4: (6, 7)}

CAUSAL_PAIRS = T * (T + 1) // 2
FLOPS = 2 * (2 * T * T * T + T * CAUSAL_PAIRS + B * P * CAUSAL_PAIRS + 2 * P * P * N)


def tile_inductionheadattentionsmaller_b_kernel(tc, table, pos, wq1, wk1, wv1, wv2, offs, out):
    nc = tc.nc

    def copy_out(turn, dst, src):
        if turn % 2 == 0:
            nc.vector.tensor_copy(dst, src)
        else:
            nc.scalar.copy(dst, src)

    with (
        tc.tile_pool(name="held", bufs=1) as held,
        tc.tile_pool(name="work", bufs=4) as work,
        tc.tile_pool(name="stats", bufs=4) as stats,
        tc.tile_pool(name="staging", bufs=4) as staging,
        tc.psum_pool(name="psum", bufs=1) as psum,
    ):

        def bank_f32(b):
            return psum.tile([P, BANK], F32, name=f"f32_bank{b}", offset=b * BANK_BYTES)

        def bank_bf16(b):
            return psum.tile([P, 2 * BANK], BF16, name=f"bf16_bank{b}", offset=b * BANK_BYTES)

        zeros = held.tile([P, P], BF16, name="zeros")
        nc.gpsimd.memset(zeros[:], 0.0)
        warm_ps = bank_f32(BANKS - 1)
        for n in range(WARM_UP_MATMULS):
            nc.tensor.matmul(warm_ps[:, 0:P], lhsT=zeros[:], rhs=zeros[:], start=True, stop=True)

        pos_sb = [held.tile([P, T], BF16, name=f"pos_sb{f}") for f in range(NB)]
        wk_sb = [held.tile([P, T], BF16, name=f"wk_sb{f}") for f in range(NB)]
        wq_sb = [held.tile([P, T], BF16, name=f"wq_sb{f}") for f in range(NB)]

        def load_pos_chunk(c):
            for f in range(NB):
                nc.sync.dma_start(pos_sb[f][:, c * BANK : (c + 1) * BANK], pos[f * P : (f + 1) * P, c * BANK : (c + 1) * BANK])

        for c in range(CHUNKS):
            nc.scalar.dma_start(wk_sb[0][:, c * BANK : (c + 1) * BANK], wk1[0:P, c * BANK : (c + 1) * BANK])
        for f in range(1, NB):
            nc.scalar.dma_start(wk_sb[f][:], wk1[f * P : (f + 1) * P, :])
        load_pos_chunk(0)
        for f in range(NB):
            queue = nc.sync if f % 2 == 0 else nc.scalar
            queue.dma_start(wq_sb[f][:], wq1[f * P : (f + 1) * P, :])
        offsets = held.tile([P, N // 16], U16, name="offsets")
        nc.sync.dma_start(offsets[:], offs)
        table_sb = held.tile([P, V], BF16, name="table_sb")
        nc.sync.dma_start(table_sb[:], table)
        wv1_sb = held.tile([P, P], BF16, name="wv1_sb")
        nc.scalar.dma_start(wv1_sb[:], wv1)
        wv2_sb = held.tile([P, P], BF16, name="wv2_sb")
        nc.scalar.dma_start(wv2_sb[:], wv2)
        load_pos_chunk(1)

        ident = held.tile([P, P], BF16, name="ident")
        make_identity(nc, ident[:])
        u_minus_t = held.tile([P, BANK], I32, name="u_minus_t")
        nc.gpsimd.iota(u_minus_t[:], pattern=[[1, BANK]], base=P - BANK, channel_multiplier=-1)
        above_diag = held.tile([P, BANK], BF16, name="above_diag")
        nc.vector.tensor_scalar(above_diag[:], u_minus_t[:], 0.0, MASKED, op0=IS_GT, op1=MULT)
        not_row0 = held.tile([P, 1], F32, name="not_row0")
        nc.vector.memset(not_row0[:], 1.0)
        nc.vector.memset(not_row0[0:1, :], 0.0)

        q_sb = [[held.tile([P, BANK], BF16, name=f"q_sb{a}_{c}") for c in range(CHUNKS)] for a in range(NB)]
        k_sb = [[held.tile([P, BANK], BF16, name=f"k_sb{a}_{c}") for c in range(CHUNKS)] for a in range(NB)]

        def project_step(acc, w_sb, a, c, f):
            nc.tensor.matmul(
                acc[:],
                lhsT=w_sb[f][:, a * P : (a + 1) * P],
                rhs=pos_sb[f][:, c * BANK : (c + 1) * BANK],
                start=(f == 0),
                stop=(f == NB - 1),
            )

        def project_together(w_sb, proj_sb, c):
            accs = [bank_f32(a) for a in range(NB)]
            for f in range(NB):
                for a in range(NB):
                    project_step(accs[a], w_sb, a, c, f)
            for a in range(NB):
                copy_out(a, proj_sb[a][c][:], accs[a][:])

        flips = []

        def weave():
            if flips:
                to, frm = flips.pop(0)
                nc.tensor.transpose(to, frm, ident[:])

        def project_row_block(w_sb, proj_sb, c, a, bank):
            acc = bank_f32(bank)
            for f in range(NB):
                project_step(acc, w_sb, a, c, f)
                weave()
            copy_out(a, proj_sb[a][c][:], acc[:])

        project_together(wk_sb, k_sb, 0)
        for a in range(NB):
            project_row_block(wq_sb, q_sb, 0, a, a)

        def looked_up(piece):
            return table_sb[:].indirect(offsets[:, piece * PIECE_COLS : (piece + 1) * PIECE_COLS])

        v1_sb = held.tile([P, N], BF16, name="v1_sb")
        for piece in range(PIECES):
            v1_ps = bank_f32(piece)
            nc.tensor.matmul(v1_ps[:], lhsT=wv1_sb[:], rhs=looked_up(piece), start=True, stop=True)
            copy_out(piece, v1_sb[:, piece * BANK : (piece + 1) * BANK], v1_ps[:])
        e_sb = held.tile([P, N], BF16, name="e_sb")
        for piece in range(PIECES):
            e_ps = bank_f32(PIECES + piece)
            nc.tensor.matmul(e_ps[:], lhsT=ident[:], rhs=looked_up(piece), start=True, stop=True)
            copy_out(piece, e_sb[:, piece * BANK : (piece + 1) * BANK], e_ps[:])

        v1T = held.tile([P, B * NB, P], BF16, name="v1T")

        def v1_flips():
            v1T_ps = [bank_bf16(T_BANKS[s]) for s in range(B)]
            for s in range(B):
                for k in range(NB):
                    flips.append((v1T_ps[s][:, k * P : (k + 1) * P], v1_sb[:, (s * NB + k) * P : (s * NB + k + 1) * P]))
            return v1T_ps

        def copy_v1T(v1T_ps):
            for s in range(B):
                copy_out(s, v1T[:, s * NB : (s + 1) * NB, :], v1T_ps[s][:].rearrange("p (k m) -> p k m", m=P))

        def scores(i, banks):
            width = (i + 1) * P
            col = (i % CHUNK_BLOCKS) * P
            bounds = [(lo, min(lo + BANK, width)) for lo in range(0, width, BANK)]
            first_woven = len(bounds) * NB - len(flips)
            pieces = []
            for p, (lo, hi) in enumerate(bounds):
                s_ps = bank_f32(banks[p])
                for a in range(NB):
                    nc.tensor.matmul(
                        s_ps[:, : hi - lo],
                        lhsT=q_sb[a][i // CHUNK_BLOCKS][:, col : col + P],
                        rhs=k_sb[a][p][:, : hi - lo],
                        start=(a == 0),
                        stop=(a == NB - 1),
                    )
                    if p * NB + a >= first_woven:
                        weave()
                pieces.append((lo, hi, s_ps[:, : hi - lo]))
            return pieces

        def softmax(i, pieces):
            width = (i + 1) * P
            two_pieces = len(pieces) == 2
            piece_max = stats.tile([P, CHUNKS], F32, name="piece_max")
            lo, hi, s = pieces[-1]
            masked = work.tile([P, BANK], F32, name="masked")
            nc.vector.tensor_tensor(out=masked[:, : hi - lo], in0=s, in1=above_diag[:, BANK - (hi - lo) :], op=ADD)
            pieces = pieces[:-1] + [(lo, hi, masked[:, : hi - lo])]
            for p, (lo, hi, s) in enumerate(pieces):
                nc.vector.reduce_max(out=piece_max[:, p : p + 1], in_=s, axis=X)
            shift = stats.tile([P, 1], F32, name="shift")
            if two_pieces:
                nc.vector.tensor_scalar(shift[:], piece_max[:, 0:1], piece_max[:, 1:2], -SCALE, op0=MAX, op1=MULT)
            else:
                nc.vector.tensor_scalar_mul(shift[:], piece_max[:, 0:1], -SCALE)
            expd = work.tile([P, T], F32, name="expd")
            piece_sum = stats.tile([P, CHUNKS], F32, name="piece_sum")
            for p, (lo, hi, s) in enumerate(pieces):
                nc.scalar.activation(
                    out=expd[:, lo:hi],
                    in_=s,
                    func=EXP,
                    bias=shift[:],
                    scale=SCALE,
                    accum_out=piece_sum[:, p : p + 1],
                )
            inv_sum = stats.tile([P, 1], F32, name="inv_sum")
            if two_pieces:
                row_sum = stats.tile([P, 1], F32, name="row_sum")
                nc.vector.tensor_add(row_sum[:], piece_sum[:, 0:1], piece_sum[:, 1:2])
                nc.vector.reciprocal(inv_sum[:], row_sum[:])
            else:
                nc.vector.reciprocal(inv_sum[:], piece_sum[:, 0:1])
            a1 = work.tile([P, T], BF16, name="a1")
            row_gate = not_row0[:] if i == 0 else 1.0
            head = pieces[0][1]
            nc.gpsimd.tensor_scalar(a1[:, :head], expd[:, :head], inv_sum[:], row_gate, op0=MULT, op1=MULT)
            if two_pieces:
                nc.scalar.activation(out=a1[:, head:width], in_=expd[:, head:width], func=COPY, scale=inv_sum[:])
            return a1

        def a1_flips(i, a1):
            a1T_ps = bank_bf16(T_BANKS[i % 2])
            for k in range(i + 1):
                flips.append((a1T_ps[:, k * P : (k + 1) * P], a1[:, k * P : (k + 1) * P]))
            return a1T_ps[:, : (i + 1) * P].rearrange("p (k t) -> p k t", t=P)

        fill = [(wk_sb, k_sb, a) for a in range(NB)] + [(wq_sb, q_sb, a) for a in range(NB)]

        def fill_row_blocks(count):
            for n in range(count):
                w_sb, proj_sb, a = fill.pop(0)
                project_row_block(w_sb, proj_sb, 1, a, FILL_BANKS[a % len(FILL_BANKS)])

        chunk_a1T = held.tile([P, CHUNK_BLOCKS, BANK], BF16, name="chunk_a1T")

        def copy_chunk_a1T(i, a1T_ps):
            nc.scalar.copy(chunk_a1T[:, : i + 1, i * P : (i + 1) * P], a1T_ps)

        a1 = None
        for i in range(CHUNK_BLOCKS - 1, -1, -1):
            pieces = scores(i, NARROW_S_BANKS[i % 2 : i % 2 + 1])
            if i == CHUNK_BLOCKS - 1:
                v1T_ps = v1_flips()
            else:
                a1T_ps = a1_flips(i + 1, a1)
            a1 = softmax(i, pieces)
            fill_row_blocks(2)
            if i == CHUNK_BLOCKS - 1:
                copy_v1T(v1T_ps)
            else:
                copy_chunk_a1T(i + 1, a1T_ps)
        a1T_ps = a1_flips(0, a1)
        fill_row_blocks(2)
        copy_chunk_a1T(0, a1T_ps)
        fill_row_blocks(len(fill))

        e_by_seq = e_sb[:].rearrange("p (s t) -> p s t", s=B)
        out_by_seq = out[0:P, :].rearrange("p (s t) -> p s t", s=B)

        def copy_a1T(i, a1T_ps):
            a1T = work.tile([P, NB, P], BF16, name="a1T")
            nc.scalar.copy(a1T[:, : i + 1, :], a1T_ps)
            return a1T

        def mix(i, a1T):
            first_woven = B * (i + 1) - len(flips)
            seqs_of_bank = B // len(Y_BANKS[i])
            for n, bank in enumerate(Y_BANKS[i]):
                y = psum.tile([P, seqs_of_bank, P], F32, name=f"y{seqs_of_bank}_bank{bank}", offset=bank * BANK_BYTES)
                first = n * seqs_of_bank
                for s in range(seqs_of_bank):
                    for k in range(i + 1):
                        nc.tensor.matmul(
                            y[:, s, :],
                            lhsT=v1T[:, (first + s) * NB + k, :],
                            rhs=a1T[:, k, :],
                            start=(k == 0),
                            stop=(k == i),
                        )
                        if (first + s) * (i + 1) + k >= first_woven:
                            weave()
                summed = staging.tile([P, seqs_of_bank, P], F32, name=f"summed{seqs_of_bank}")
                there = (slice(None), slice(first, first + seqs_of_bank), slice(i * P, (i + 1) * P))
                nc.vector.tensor_tensor(out=summed[:], in0=y[:], in1=e_by_seq[there], op=ADD)
                nc.sync.dma_start(out_by_seq[there], summed[:])

        def mix_chunk(s):
            y = bank_f32(CHUNK_Y_BANKS[s])
            for k in range(CHUNK_BLOCKS):
                nc.tensor.matmul(
                    y[:, k * P :],
                    lhsT=v1T[:, s * NB + k, :],
                    rhs=chunk_a1T[:, k, k * P :],
                    start=(k == 0),
                    stop=(k == CHUNK_BLOCKS - 1),
                )
            summed = staging.tile([P, BANK], F32, name="summed_chunk")
            nc.vector.tensor_tensor(out=summed[:], in0=y[:], in1=e_sb[:, s * T : s * T + BANK], op=ADD)
            nc.sync.dma_start(out[0:P, s * T : s * T + BANK], summed[:])

        def project_v2():
            for piece in range(PIECES):
                v2_ps = bank_f32(V2_BANKS[piece])
                nc.tensor.matmul(v2_ps[:], lhsT=wv2_sb[:], rhs=looked_up(piece), start=True, stop=True)
                if piece >= PIECES // 2:
                    for n in range(3):
                        weave()
                v2_sb = staging.tile([P, BANK], F32, name="staged")
                copy_out(1 if piece < PIECES // 2 else 0, v2_sb[:], v2_ps[:])
                nc.sync.dma_start(out[P : 2 * P, piece * BANK : (piece + 1) * BANK], v2_sb[:])

        a1_of = {}
        a1T_of = {}
        for i in range(NB - 1, CHUNK_BLOCKS - 1, -1):
            if i + 2 < NB:
                a1T_ps = a1_flips(i + 2, a1_of[i + 2])
            pieces = scores(i, WIDE_S_BANKS[i % 2])
            if i + 2 < NB:
                a1T_of[i + 2] = copy_a1T(i + 2, a1T_ps)
            a1_of[i] = softmax(i, pieces)

        mix(7, a1T_of[7])
        a1T_ps = a1_flips(5, a1_of[5])
        project_v2()
        a1T_of[5] = copy_a1T(5, a1T_ps)
        mix_chunk(0)
        mix_chunk(1)
        a1T_ps = a1_flips(4, a1_of[4])
        mix(6, a1T_of[6])
        a1T_of[4] = copy_a1T(4, a1T_ps)
        mix(5, a1T_of[5])
        mix(4, a1T_of[4])
